import numpy as np
import ml_dtypes


def mxq(x, axis, fmt="e4m3"):
    dtype, down = {"e4m3": (ml_dtypes.float8_e4m3fn, 7), "e5m2": (ml_dtypes.float8_e5m2, 14)}[fmt]
    v = np.moveaxis(np.asarray(x, np.float32).astype(ml_dtypes.bfloat16).astype(np.float64), axis, -1)
    blocks = v.reshape(v.shape[:-1] + (-1, 32))
    amax = np.abs(blocks).max(-1, keepdims=True)
    byte = np.maximum(np.where(amax > 0, np.frexp(amax)[1] - 1 + 127, 0) - down, 1)
    scale = np.exp2(byte - 127.0)
    codes = (blocks / scale).astype(np.float32).astype(dtype).astype(np.float64)
    return np.moveaxis((codes * scale).reshape(v.shape), -1, axis)


WIDE = False


def mx_kscale(k):
    if not WIDE:
        return np.ones(k)
    levels = np.array([10, -10, 5, -5, 0])
    a = np.random.permutation(np.resize(levels, k // 512 * 4)).reshape(k // 512, 4)
    idx = np.arange(k)
    return np.exp2(a[idx // 512, idx % 128 // 32])


BF16 = ml_dtypes.bfloat16


def bf(x):
    return np.asarray(x, np.float32).astype(BF16)


def f64(x):
    return np.asarray(x).astype(np.float64)


E2M1 = np.array([0.0, 0.5, 1.0, 1.5, 2.0, 3.0, 4.0, 6.0, -0.0, -0.5, -1.0, -1.5, -2.0, -3.0, -4.0, -6.0])


def pack_weight(w, fmt):
    k, n = w.shape
    w = f64(bf(w)).reshape(k // 32, 32, n)
    amax = np.abs(w).max(1)
    if fmt == "e4m3":
        byte = np.frexp(amax)[1] - 1 + 127 - 7
    else:
        mant, ex = np.frexp(amax / 6.0)
        byte = np.where(mant > 0.5, ex, ex - 1) + 127
    byte = np.clip(np.where(amax > 0, byte, 1), 1, 254)
    scaled = (w * np.exp2(127.0 - byte)[:, None, :]).reshape(k, n).astype(np.float32)
    by_word = np.ascontiguousarray(scaled.reshape(k // 512, 128, 4, n).transpose(0, 1, 3, 2))
    if fmt == "e4m3":
        words = by_word.astype(ml_dtypes.float8_e4m3fn).view(np.uint8)
    else:
        c = by_word.astype(ml_dtypes.float4_e2m1fn).view(np.uint8) & 0xF
        words = c[..., 0::2] | (c[..., 1::2] << 4)
    return np.ascontiguousarray(words), np.ascontiguousarray(byte.astype(np.uint8).reshape(k // 512, 16, n))


def unpack_weight(words, scales, fmt):
    g, p, n, _ = words.shape
    if fmt == "e4m3":
        vals = np.ascontiguousarray(words).view(ml_dtypes.float8_e4m3fn).astype(np.float64)
    else:
        nib = np.empty((g, p, n, 4), np.uint8)
        nib[..., 0::2] = words & 0xF
        nib[..., 1::2] = words >> 4
        vals = E2M1[nib]
    vals = vals * np.repeat(np.exp2(scales.astype(np.float64) - 127.0), 8, axis=1)[..., None]
    return vals.transpose(0, 1, 3, 2).reshape(g * 512, n)


B, DETER, STOCH, ACT, HID, BLOCKS, NIN, NG = 4096, 512, 1024, 512, 512, 1, 3, 3
DPB = DETER // BLOCKS
EPS = 1e-4


def silu(v):
    return v / (1.0 + np.exp(-v))


def sigmoid(v):
    return 1.0 / (1.0 + np.exp(-v))


def rmsnorm(v, g):
    return v * (1.0 / np.sqrt(np.mean(v * v, axis=-1, keepdims=True) + EPS)) * g


def setup_inputs():
    s = mx_kscale(DETER)
    n = np.random.standard_normal
    hid0 = bf(silu(n((B, DETER))) * s)
    deter = bf(n((B, DETER)))
    hw1 = n((BLOCKS, DPB, DPB)) * 1.5 / np.sqrt(DPB) / s.reshape(BLOCKS, DPB, 1)
    hw1_words, hw1_scales = pack_weight(hw1.reshape(-1, DPB), "e4m3")
    hb1 = bf(n(DETER) * 0.1)
    hg1 = bf(1.0 + n(DETER) * 0.1)
    gw = n((BLOCKS, DPB, NG * DPB)) * 2.0 / np.sqrt(DPB)
    gw_words, gw_scales = pack_weight(gw.reshape(-1, NG * DPB), "e4m3")
    gb = bf(n(NG * DETER) * 0.2)
    return {"hid0": hid0, "deter": deter,
            "hw1_words": hw1_words, "hw1_scales": hw1_scales, "hb1": hb1, "hg1": hg1,
            "gw_words": gw_words, "gw_scales": gw_scales, "gb": gb}


def block_linear(vq, wq, b):
    y = vq.transpose(1, 0, 2) @ wq
    return y.transpose(1, 0, 2).reshape(B, -1) + b


def reference(hid0, deter, hw1_words, hw1_scales, hb1, hg1, gw_words, gw_scales, gb):
    u = block_linear(mxq(f64(hid0).reshape(B, BLOCKS, DPB), 2, "e4m3"), unpack_weight(hw1_words, hw1_scales, "e4m3").reshape(BLOCKS, DPB, DPB), f64(hb1))
    h = silu(rmsnorm(u, f64(hg1)))
    p = block_linear(mxq(h.reshape(B, BLOCKS, DPB), 2, "e4m3"), unpack_weight(gw_words, gw_scales, "e4m3").reshape(BLOCKS, DPB, NG * DPB), f64(gb))
    g = p.reshape(B, BLOCKS, NG, DPB)
    reset = sigmoid(g[:, :, 0, :].reshape(B, DETER))
    cand = np.tanh(reset * g[:, :, 1, :].reshape(B, DETER))
    update = sigmoid(g[:, :, 2, :].reshape(B, DETER) - 1.0)
    return update * cand + (1.0 - update) * f64(deter)

@@ -1,0 +1,336 @@
+import concourse.mybir as mybir
+from concourse.masks import make_identity
+
+F32 = mybir.dt.float32
+BF16 = mybir.dt.bfloat16
+I32 = mybir.dt.int32
+U32 = mybir.dt.uint32
+U8 = mybir.dt.uint8
+FP8X4 = mybir.dt.float8_e4m3fn_x4
+ACT = mybir.ActivationFunctionType
+ALU = mybir.AluOpType
+
+P = 128
+PACK = 4
+ROWS = 4096
+WIDTH = 512
+GATES = 3
+EPS = 1e-4
+
+TILES = ROWS // P
+PAIRS = TILES // 2
+CHUNK = 4
+SLICES = WIDTH // P
+UNITS = (TILES // CHUNK) * SLICES
+OUT_LAG = 6
+
+FLOPS = 2 * ROWS * WIDTH * (WIDTH + GATES * WIDTH)
+
+
+def load_scale_rows(nc, plane, scales):
+    for quadrant in range(4):
+        nc.sync.dma_start(
+            out=plane[32 * quadrant : 32 * quadrant + 4, :].bitcast(I32),
+            in_=scales[0, 4 * quadrant : 4 * quadrant + 4, :].bitcast(I32),
+        )
+
+
+def tile_deter_pb_t_e_kernel(
+    tc, hid0, deter, hw1_words, hw1_scales, hb1, hg1, gw_words, gw_scales, gb, out
+):
+    nc = tc.nc
+    hid_rows = hid0.rearrange("(r i) k -> r i k", i=TILES)
+    det_rows = deter.rearrange("(r i) n -> r i n", i=TILES)
+    out_rows = out.rearrange("(r i) n -> r i n", i=TILES)
+
+    with tc.tile_pool(name="keep", bufs=1) as keep, tc.tile_pool(
+        name="work", bufs=3
+    ) as work, tc.manual_schedule():
+        x_sb = keep.tile([P, TILES, WIDTH], BF16, name="x_sb")
+        det_sb = keep.tile([P, TILES, WIDTH], BF16, name="det_sb")
+        hw_codes = keep.tile([P, WIDTH], U32, name="hw_codes", align_bytes=64)
+        hw_plane = keep.tile([P, WIDTH], U8, name="hw_plane", align_bytes=64)
+        gw_codes = keep.tile([P, GATES * WIDTH], U32, name="gw_codes", align_bytes=64)
+        gw_plane = keep.tile([P, GATES * WIDTH], U8, name="gw_plane", align_bytes=64)
+        x_codes = keep.tile([P, ROWS], U32, name="x_codes", align_bytes=64)
+        x_plane = keep.tile([P, ROWS], U8, name="x_plane", align_bytes=64)
+        h_codes = keep.tile([P, ROWS], U32, name="h_codes", align_bytes=64)
+        h_plane = keep.tile([P, ROWS], U8, name="h_plane", align_bytes=64)
+        ident_f = keep.tile([P, P], F32, name="ident_f")
+        ident_b = keep.tile([P, P], BF16, name="ident_b")
+        gb_rows = keep.tile([P, P], BF16, name="gb_rows")
+        gate_bias = keep.tile([P, GATES * SLICES], F32, name="gate_bias")
+        hb_all = keep.tile([P, WIDTH], BF16, name="hb_all")
+        hg_all = keep.tile([P, WIDTH], BF16, name="hg_all")
+        bias_tq = keep.tile([P, PACK, P], F32, name="bias_tq")
+        gain_tq = keep.tile([P, PACK, P], F32, name="gain_tq")
+        sum_sq = keep.tile([P, TILES], F32, name="sum_sq")
+        mean_sq = keep.tile([P, TILES], F32, name="mean_sq")
+        inv_rms = keep.tile([P, TILES], F32, name="inv_rms")
+        minus_half = keep.tile([P, 1], F32, name="minus_half")
+
+        nc.vector.memset(hw_plane[:].bitcast(I32), 0)
+        nc.vector.memset(gw_plane[:].bitcast(I32), 0)
+        nc.gpsimd.memset(gb_rows[:], 0.0)
+        nc.gpsimd.memset(minus_half[:], -0.5)
+        make_identity(nc, ident_b[:])
+        make_identity(nc, ident_f[:])
+
+        nc.scalar.dma_start(out=hb_all[:], in_=hb1.partition_broadcast(P))
+        nc.scalar.dma_start(out=hg_all[:], in_=hg1.partition_broadcast(P))
+        nc.sync.dma_start(
+            out=gb_rows[0 : GATES * SLICES, :], in_=gb.rearrange("(a m) -> a m", m=P)
+        )
+        nc.sync.dma_start(out=x_sb[:, 0:CHUNK, :], in_=hid_rows[:, 0:CHUNK, :])
+        nc.sync.dma_start(
+            out=hw_codes[:].bitcast(I32),
+            in_=hw1_words.rearrange("g p n t -> (g p) (n t)").bitcast(I32),
+        )
+        load_scale_rows(nc, hw_plane, hw1_scales)
+        for first in range(CHUNK, TILES, CHUNK):
+            nc.sync.dma_start(
+                out=x_sb[:, first : first + CHUNK, :], in_=hid_rows[:, first : first + CHUNK, :]
+            )
+        nc.sync.dma_start(
+            out=gw_codes[:].bitcast(I32),
+            in_=gw_words.rearrange("g p n t -> (g p) (n t)").bitcast(I32),
+        )
+        load_scale_rows(nc, gw_plane, gw_scales)
+        for first in range(0, TILES, 2 * CHUNK):
+            nc.sync.dma_start(
+                out=det_sb[:, first : first + 2 * CHUNK, :],
+                in_=det_rows[:, first : first + 2 * CHUNK, :],
+            )
+
+        nc.vector.tensor_copy(out=bias_tq[:], in_=hb_all[:].rearrange("r (q t) -> r t q", t=PACK))
+        nc.vector.tensor_copy(out=gain_tq[:], in_=hg_all[:].rearrange("r (q t) -> r t q", t=PACK))
+
+        with tc.psum_pool(name="psum_hidden", bufs=1) as psum:
+            gb_t = psum.tile([P, P], BF16, name="gb_t")
+            nc.tensor.transpose(gb_t[:], gb_rows[:], ident_b[:])
+            nc.vector.tensor_copy(out=gate_bias[:, 0 : 2 * SLICES], in_=gb_t[:, 0 : 2 * SLICES])
+            nc.vector.tensor_scalar_add(
+                out=gate_bias[:, 2 * SLICES : 3 * SLICES],
+                in0=gb_t[:, 2 * SLICES : 3 * SLICES],
+                scalar1=-1.0,
+            )
+
+            x_t, x_grouped, u_psum, u_sb, w_sb, w_t, h_grouped = {}, {}, {}, {}, {}, {}, {}
+
+            def transpose_hid(pair):
+                x_t[pair] = psum.tile([P, 2, 2, P], F32, name="x_t", bufs=2)
+                for a in range(2):
+                    words = x_sb[:, 2 * pair + a, :].bitcast(F32)
+                    for v in range(2):
+                        nc.tensor.transpose(x_t[pair][:, a, v, :], words[:, v : WIDTH // 2 : 2], ident_f[:])
+
+            def group_hid(pair):
+                x_grouped[pair] = work.tile([P, 2, P, PACK], BF16, name="x_grouped", align_bytes=64)
+                nc.scalar.copy(
+                    out=x_grouped[pair][:].bitcast(F32),
+                    in_=x_t[pair][:].rearrange("p a v r -> p a r v"),
+                )
+
+            def quantise_pair(grouped, codes, plane, pair):
+                cols = slice(2 * P * pair, 2 * P * (pair + 1))
+                nc.vector.quantize_mx(
+                    out=codes[:, cols].bitcast(FP8X4),
+                    scales=plane[:, cols],
+                    in_=grouped[pair][:].rearrange("p a r t -> p (a r t)"),
+                )
+
+            def hidden_matmul(i):
+                rows = slice(P * i, P * (i + 1))
+                u_psum[i] = psum.tile([P, WIDTH], F32, name="u_psum", bufs=2)
+                nc.tensor.matmul_mx(
+                    out=u_psum[i][:],
+                    lhsT=x_codes[:, rows].bitcast(FP8X4),
+                    lhsT_scale=x_plane[:, rows],
+                    rhs=hw_codes[:].bitcast(FP8X4),
+                    rhs_scale=hw_plane[:],
+                    start=True,
+                    stop=True,
+                )
+
+            def add_bias(i):
+                u_sb[i] = work.tile([P, PACK, P], F32, name="u_sb", bufs=5)
+                nc.vector.tensor_tensor(
+                    out=u_sb[i][:],
+                    in0=u_psum[i][:].rearrange("r (q t) -> r t q", t=PACK),
+                    in1=bias_tq[:],
+                    op=ALU.add,
+                )
+
+            def sum_squares(i):
+                squares = work.tile([P, WIDTH], BF16, name="squares", bufs=4)
+                nc.scalar.activation(
+                    out=squares[:],
+                    in_=u_sb[i][:].rearrange("r t q -> r (t q)"),
+                    func=ACT.Square,
+                    accum_out=sum_sq[:, i : i + 1],
+                )
+
+            def inverse_rms(i):
+                one = slice(i, i + 1)
+                nc.gpsimd.tensor_scalar(
+                    out=mean_sq[:, one], in0=sum_sq[:, one],
+                    scalar1=1.0 / WIDTH, scalar2=EPS, op0=ALU.mult, op1=ALU.add,
+                )
+                nc.gpsimd.tensor_tensor(
+                    out=inv_rms[:, one], in0=mean_sq[:, one], in1=minus_half[:], op=ALU.pow
+                )
+
+            def normalise(i):
+                w_sb[i] = work.tile([P, PACK, P], F32, name="w_sb")
+                nc.vector.scalar_tensor_tensor(
+                    out=w_sb[i][:].rearrange("r t q -> r (t q)"),
+                    in0=u_sb[i][:].rearrange("r t q -> r (t q)"),
+                    scalar=inv_rms[:, i : i + 1],
+                    in1=gain_tq[:].rearrange("r t q -> r (t q)"),
+                    op0=ALU.mult,
+                    op1=ALU.mult,
+                )
+
+            def transpose_normalised(i):
+                w_t[i] = psum.tile([P, PACK, P], F32, name="w_t", bufs=3)
+                for t in range(PACK):
+                    nc.tensor.transpose(w_t[i][:, t, :], w_sb[i][:, t, :], ident_f[:])
+
+            def silu_and_group(i):
+                if i % 2 == 0:
+                    h_grouped[i // 2] = work.tile([P, 2, P, PACK], BF16, name="h_grouped", align_bytes=64)
+                nc.scalar.activation(
+                    out=h_grouped[i // 2][:, i % 2, :, :],
+                    in_=w_t[i][:].rearrange("q t r -> q r t"),
+                    func=ACT.Silu,
+                )
+
+            for step in range(-4, TILES + 4):
+                if 0 <= step + 1 < TILES:
+                    hidden_matmul(step + 1)
+                if 0 <= step < TILES:
+                    add_bias(step)
+                if 0 <= step - 1 < TILES:
+                    sum_squares(step - 1)
+                    inverse_rms(step - 1)
+                if 0 <= step - 2 < TILES:
+                    normalise(step - 2)
+                    transpose_normalised(step - 2)
+                if 0 <= step - 3 < TILES:
+                    silu_and_group(step - 3)
+                if step % 2 == 0 and 0 <= (step + 4) // 2 < PAIRS:
+                    transpose_hid((step + 4) // 2)
+                if step % 2 == 1 and 0 <= (step + 3) // 2 < PAIRS:
+                    group_hid((step + 3) // 2)
+                if step % 2 == 0 and 0 <= (step + 2) // 2 < PAIRS:
+                    quantise_pair(x_grouped, x_codes, x_plane, (step + 2) // 2)
+                if step % 2 == 1 and 0 <= (step - 5) // 2 < PAIRS:
+                    quantise_pair(h_grouped, h_codes, h_plane, (step - 5) // 2)
+
+        with tc.psum_pool(name="psum_gru", bufs=1, reuse_waits="tile") as psum:
+            gate_psum, det_t, reset, product, update, cand, mixed, back = {}, {}, {}, {}, {}, {}, {}, {}
+
+            def gate_matmul(unit, gate):
+                chunk, j = divmod(unit, SLICES)
+                cols = slice(WIDTH * gate + P * j, WIDTH * gate + P * (j + 1))
+                rows = slice(CHUNK * P * chunk, CHUNK * P * (chunk + 1))
+                gate_psum[unit, gate] = psum.tile([P, CHUNK * P], F32, name="gate_psum", bufs=5)
+                nc.tensor.matmul_mx(
+                    out=gate_psum[unit, gate][:],
+                    lhsT=gw_codes[:, cols].bitcast(FP8X4),
+                    lhsT_scale=gw_plane[:, cols],
+                    rhs=h_codes[:, rows].bitcast(FP8X4),
+                    rhs_scale=h_plane[:, rows],
+                    start=True,
+                    stop=True,
+                )
+
+            def bias_of(unit, gate):
+                column = SLICES * gate + unit % SLICES
+                return gate_bias[:, column : column + 1]
+
+            def transpose_deter(first_unit):
+                det_t[first_unit // 2] = psum.tile([P, 2, CHUNK, P], BF16, name="det_t", bufs=1)
+                for unit in (first_unit, first_unit + 1):
+                    chunk, j = divmod(unit, SLICES)
+                    for a in range(CHUNK):
+                        nc.tensor.transpose(
+                            det_t[first_unit // 2][:, unit % 2, a, :],
+                            det_sb[:, CHUNK * chunk + a, P * j : P * (j + 1)],
+                            ident_b[:],
+                        )
+
+            def reset_gate(unit):
+                reset[unit] = work.tile([P, CHUNK * P], F32, name="reset")
+                nc.scalar.activation(
+                    out=reset[unit][:], in_=gate_psum[unit, 0][:], func=ACT.Sigmoid, bias=bias_of(unit, 0)
+                )
+
+            def reset_times_c(unit):
+                product[unit] = work.tile([P, CHUNK * P], F32, name="product")
+                nc.vector.scalar_tensor_tensor(
+                    out=product[unit][:],
+                    in0=gate_psum[unit, 1][:],
+                    scalar=bias_of(unit, 1),
+                    in1=reset[unit][:],
+                    op0=ALU.add,
+                    op1=ALU.mult,
+                )
+
+            def update_gate(unit):
+                update[unit] = work.tile([P, CHUNK * P], F32, name="update", bufs=4)
+                nc.scalar.activation(
+                    out=update[unit][:], in_=gate_psum[unit, 2][:], func=ACT.Sigmoid, bias=bias_of(unit, 2)
+                )
+
+            def candidate(unit):
+                cand[unit] = work.tile([P, CHUNK * P], F32, name="cand")
+                nc.scalar.activation(out=cand[unit][:], in_=product[unit][:], func=ACT.Tanh)
+
+            def mix(unit):
+                chunk, j = divmod(unit, SLICES)
+                if j == 0:
+                    mixed[chunk] = work.tile([P, SLICES, CHUNK * P], F32, name="mixed")
+                diff = work.tile([P, CHUNK * P], F32, name="diff")
+                nc.vector.tensor_tensor(
+                    out=diff[:],
+                    in0=cand[unit][:],
+                    in1=det_t[unit // 2][:, unit % 2, :, :].rearrange("n a r -> n (a r)"),
+                    op=ALU.subtract,
+                )
+                nc.gpsimd.tensor_tensor(
+                    out=mixed[chunk][:, j, :], in0=update[unit][:], in1=diff[:], op=ALU.mult
+                )
+
+            def transpose_back(i):
+                chunk, a = divmod(i, CHUNK)
+                back[i] = psum.tile([P, WIDTH], F32, name="back", bufs=2)
+                for j in range(SLICES):
+                    nc.tensor.transpose(
+                        back[i][:, P * j : P * (j + 1)], mixed[chunk][:, j, P * a : P * (a + 1)], ident_f[:]
+                    )
+
+            def add_deter_and_store(i):
+                result = work.tile([P, WIDTH], F32, name="result", bufs=4)
+                nc.vector.tensor_tensor(out=result[:], in0=back[i][:], in1=det_sb[:, i, :], op=ALU.add)
+                nc.sync.dma_start(out=out_rows[:, i, :], in_=result[:])
+
+            for step in range(-1, UNITS + OUT_LAG):
+                if 0 <= step - 2 < UNITS:
+                    mix(step - 2)
+                if 0 <= step - OUT_LAG < TILES:
+                    transpose_back(step - OUT_LAG)
+                if step % 2 == 1 and 0 <= step - 1 < UNITS:
+                    transpose_deter(step - 1)
+                if 0 <= step < UNITS:
+                    reset_gate(step)
+                if 0 <= step + 1 < UNITS:
+                    for gate in range(GATES):
+                        gate_matmul(step + 1, gate)
+                if 0 <= step < UNITS:
+                    reset_times_c(step)
+                    update_gate(step)
+                if 0 <= step - 1 < UNITS:
+                    candidate(step - 1)
+                if 0 <= step - OUT_LAG < TILES:
+                    add_deter_and_store(step - OUT_LAG)

@@ -22,7 +22,7 @@ PAIRS = TILES // 2
 CHUNK = 4
 SLICES = WIDTH // P
 UNITS = (TILES // CHUNK) * SLICES
-OUT_LAG = 6
+OUT_LAG = 4
 
 FLOPS = 2 * ROWS * WIDTH * (WIDTH + GATES * WIDTH)
 
@@ -118,7 +118,7 @@ def tile_deter_pb_t_e_kernel(
             x_t, x_grouped, u_psum, u_sb, w_sb, w_t, h_grouped = {}, {}, {}, {}, {}, {}, {}
 
             def transpose_hid(pair):
-                x_t[pair] = psum.tile([P, 2, 2, P], F32, name="x_t", bufs=2)
+                x_t[pair] = psum.tile([P, 2, 2, P], F32, name="x_t", bufs=1)
                 for a in range(2):
                     words = x_sb[:, 2 * pair + a, :].bitcast(F32)
                     for v in range(2):
@@ -141,7 +141,7 @@ def tile_deter_pb_t_e_kernel(
 
             def hidden_matmul(i):
                 rows = slice(P * i, P * (i + 1))
-                u_psum[i] = psum.tile([P, WIDTH], F32, name="u_psum", bufs=2)
+                u_psum[i] = psum.tile([P, WIDTH], F32, name="u_psum", bufs=3)
                 nc.tensor.matmul_mx(
                     out=u_psum[i][:],
                     lhsT=x_codes[:, rows].bitcast(FP8X4),
@@ -206,8 +206,11 @@ def tile_deter_pb_t_e_kernel(
                 )
 
             for step in range(-4, TILES + 4):
-                if 0 <= step + 1 < TILES:
+                if step % 2 == 1 and 0 <= step + 1 < TILES:
                     hidden_matmul(step + 1)
+                    hidden_matmul(step + 2)
+                if step % 2 == 0 and 0 <= (step + 4) // 2 < PAIRS:
+                    transpose_hid((step + 4) // 2)
                 if 0 <= step < TILES:
                     add_bias(step)
                 if 0 <= step - 1 < TILES:
@@ -218,8 +221,6 @@ def tile_deter_pb_t_e_kernel(
                     transpose_normalised(step - 2)
                 if 0 <= step - 3 < TILES:
                     silu_and_group(step - 3)
-                if step % 2 == 0 and 0 <= (step + 4) // 2 < PAIRS:
-                    transpose_hid((step + 4) // 2)
                 if step % 2 == 1 and 0 <= (step + 3) // 2 < PAIRS:
                     group_hid((step + 3) // 2)
                 if step % 2 == 0 and 0 <= (step + 2) // 2 < PAIRS:
@@ -234,7 +235,7 @@ def tile_deter_pb_t_e_kernel(
                 chunk, j = divmod(unit, SLICES)
                 cols = slice(WIDTH * gate + P * j, WIDTH * gate + P * (j + 1))
                 rows = slice(CHUNK * P * chunk, CHUNK * P * (chunk + 1))
-                gate_psum[unit, gate] = psum.tile([P, CHUNK * P], F32, name="gate_psum", bufs=5)
+                gate_psum[unit, gate] = psum.tile([P, CHUNK * P], F32, name="gate_psum", bufs=4)
                 nc.tensor.matmul_mx(
                     out=gate_psum[unit, gate][:],
                     lhsT=gw_codes[:, cols].bitcast(FP8X4),
@@ -249,16 +250,15 @@ def tile_deter_pb_t_e_kernel(
                 column = SLICES * gate + unit % SLICES
                 return gate_bias[:, column : column + 1]
 
-            def transpose_deter(first_unit):
-                det_t[first_unit // 2] = psum.tile([P, 2, CHUNK, P], BF16, name="det_t", bufs=1)
-                for unit in (first_unit, first_unit + 1):
-                    chunk, j = divmod(unit, SLICES)
-                    for a in range(CHUNK):
-                        nc.tensor.transpose(
-                            det_t[first_unit // 2][:, unit % 2, a, :],
-                            det_sb[:, CHUNK * chunk + a, P * j : P * (j + 1)],
-                            ident_b[:],
-                        )
+            def transpose_deter(unit):
+                chunk, j = divmod(unit, SLICES)
+                det_t[unit] = psum.tile([P, CHUNK, P], BF16, name="det_t", bufs=2)
+                for a in range(CHUNK):
+                    nc.tensor.transpose(
+                        det_t[unit][:, a, :],
+                        det_sb[:, CHUNK * chunk + a, P * j : P * (j + 1)],
+                        ident_b[:],
+                    )
 
             def reset_gate(unit):
                 reset[unit] = work.tile([P, CHUNK * P], F32, name="reset")
@@ -288,49 +288,55 @@ def tile_deter_pb_t_e_kernel(
                 nc.scalar.activation(out=cand[unit][:], in_=product[unit][:], func=ACT.Tanh)
 
             def mix(unit):
-                chunk, j = divmod(unit, SLICES)
-                if j == 0:
-                    mixed[chunk] = work.tile([P, SLICES, CHUNK * P], F32, name="mixed")
+                mixed[unit] = work.tile([P, CHUNK, P], F32, name="mixed", bufs=4)
                 diff = work.tile([P, CHUNK * P], F32, name="diff")
                 nc.vector.tensor_tensor(
                     out=diff[:],
                     in0=cand[unit][:],
-                    in1=det_t[unit // 2][:, unit % 2, :, :].rearrange("n a r -> n (a r)"),
+                    in1=det_t[unit][:].rearrange("n a r -> n (a r)"),
                     op=ALU.subtract,
                 )
                 nc.gpsimd.tensor_tensor(
-                    out=mixed[chunk][:, j, :], in0=update[unit][:], in1=diff[:], op=ALU.mult
+                    out=mixed[unit][:].rearrange("n a r -> n (a r)"),
+                    in0=update[unit][:],
+                    in1=diff[:],
+                    op=ALU.mult,
                 )
 
-            def transpose_back(i):
-                chunk, a = divmod(i, CHUNK)
-                back[i] = psum.tile([P, WIDTH], F32, name="back", bufs=2)
-                for j in range(SLICES):
-                    nc.tensor.transpose(
-                        back[i][:, P * j : P * (j + 1)], mixed[chunk][:, j, P * a : P * (a + 1)], ident_f[:]
-                    )
+            def transpose_back(unit):
+                back[unit] = psum.tile([P, CHUNK, P], F32, name="back", bufs=2)
+                for a in range(CHUNK):
+                    nc.tensor.transpose(back[unit][:, a, :], mixed[unit][:, a, :], ident_f[:])
 
-            def add_deter_and_store(i):
-                result = work.tile([P, WIDTH], F32, name="result", bufs=4)
-                nc.vector.tensor_tensor(out=result[:], in0=back[i][:], in1=det_sb[:, i, :], op=ALU.add)
-                nc.sync.dma_start(out=out_rows[:, i, :], in_=result[:])
+            def add_deter_and_store(unit):
+                chunk, j = divmod(unit, SLICES)
+                tiles = slice(CHUNK * chunk, CHUNK * (chunk + 1))
+                cols = slice(P * j, P * (j + 1))
+                result = work.tile([P, CHUNK, P], F32, name="result", bufs=4)
+                nc.vector.tensor_tensor(
+                    out=result[:], in0=back[unit][:], in1=det_sb[:, tiles, cols], op=ALU.add
+                )
+                nc.sync.dma_start(out=out_rows[:, tiles, cols], in_=result[:])
 
             for step in range(-1, UNITS + OUT_LAG):
                 if 0 <= step - 2 < UNITS:
                     mix(step - 2)
-                if 0 <= step - OUT_LAG < TILES:
+                if 0 <= step - OUT_LAG < UNITS:
                     transpose_back(step - OUT_LAG)
-                if step % 2 == 1 and 0 <= step - 1 < UNITS:
+                if 0 <= step - 1 < UNITS:
                     transpose_deter(step - 1)
                 if 0 <= step < UNITS:
                     reset_gate(step)
                 if 0 <= step + 1 < UNITS:
-                    for gate in range(GATES):
-                        gate_matmul(step + 1, gate)
+                    gate_matmul(step + 1, 0)
+                    gate_matmul(step + 1, 1)
                 if 0 <= step < UNITS:
                     reset_times_c(step)
+                if 0 <= step + 1 < UNITS:
+                    gate_matmul(step + 1, 2)
+                if 0 <= step < UNITS:
                     update_gate(step)
                 if 0 <= step - 1 < UNITS:
                     candidate(step - 1)
-                if 0 <= step - OUT_LAG < TILES:
+                if 0 <= step - OUT_LAG < UNITS:
                     add_deter_and_store(step - OUT_LAG)

@@ -52,8 +52,7 @@ def tile_deter_pb_t_e_kernel(
         hw_plane = keep.tile([P, WIDTH], U8, name="hw_plane", align_bytes=64)
         gw_codes = keep.tile([P, GATES * WIDTH], U32, name="gw_codes", align_bytes=64)
         gw_plane = keep.tile([P, GATES * WIDTH], U8, name="gw_plane", align_bytes=64)
-        x_codes = keep.tile([P, ROWS], U32, name="x_codes", align_bytes=64)
-        x_plane = keep.tile([P, ROWS], U8, name="x_plane", align_bytes=64)
+        h_grouped = keep.tile([P, TILES, P, PACK], BF16, name="h_grouped", align_bytes=64)
         h_codes = keep.tile([P, ROWS], U32, name="h_codes", align_bytes=64)
         h_plane = keep.tile([P, ROWS], U8, name="h_plane", align_bytes=64)
         ident_f = keep.tile([P, P], F32, name="ident_f")
@@ -81,12 +80,13 @@ def tile_deter_pb_t_e_kernel(
         nc.sync.dma_start(
             out=gb_rows[0 : GATES * SLICES, :], in_=gb.rearrange("(a m) -> a m", m=P)
         )
-        nc.sync.dma_start(out=x_sb[:, 0:CHUNK, :], in_=hid_rows[:, 0:CHUNK, :])
+        nc.sync.dma_start(out=x_sb[:, 0:2, :], in_=hid_rows[:, 0:2, :])
         nc.sync.dma_start(
             out=hw_codes[:].bitcast(I32),
             in_=hw1_words.rearrange("g p n t -> (g p) (n t)").bitcast(I32),
         )
         load_scale_rows(nc, hw_plane, hw1_scales)
+        nc.sync.dma_start(out=x_sb[:, 2:CHUNK, :], in_=hid_rows[:, 2:CHUNK, :])
         for first in range(CHUNK, TILES, CHUNK):
             nc.sync.dma_start(
                 out=x_sb[:, first : first + CHUNK, :], in_=hid_rows[:, first : first + CHUNK, :]
@@ -106,7 +106,7 @@ def tile_deter_pb_t_e_kernel(
         nc.vector.tensor_copy(out=gain_tq[:], in_=hg_all[:].rearrange("r (q t) -> r t q", t=PACK))
 
         with tc.psum_pool(name="psum_hidden", bufs=1) as psum:
-            gb_t = psum.tile([P, P], BF16, name="gb_t")
+            gb_t = psum.tile([P, P], BF16, name="gb_t", tag="x_t", bufs=2)
             nc.tensor.transpose(gb_t[:], gb_rows[:], ident_b[:])
             nc.vector.tensor_copy(out=gate_bias[:, 0 : 2 * SLICES], in_=gb_t[:, 0 : 2 * SLICES])
             nc.vector.tensor_scalar_add(
@@ -115,10 +115,10 @@ def tile_deter_pb_t_e_kernel(
                 scalar1=-1.0,
             )
 
-            x_t, x_grouped, u_psum, u_sb, w_sb, w_t, h_grouped = {}, {}, {}, {}, {}, {}, {}
+            x_t, x_grouped, x_codes, x_plane, u_psum, u_sb, w_sb, w_t = {}, {}, {}, {}, {}, {}, {}, {}
 
             def transpose_hid(pair):
-                x_t[pair] = psum.tile([P, 2, 2, P], F32, name="x_t", bufs=1)
+                x_t[pair] = psum.tile([P, 2, 2, P], F32, name="x_t", bufs=2)
                 for a in range(2):
                     words = x_sb[:, 2 * pair + a, :].bitcast(F32)
                     for v in range(2):
@@ -131,21 +131,22 @@ def tile_deter_pb_t_e_kernel(
                     in_=x_t[pair][:].rearrange("p a v r -> p a r v"),
                 )
 
-            def quantise_pair(grouped, codes, plane, pair):
-                cols = slice(2 * P * pair, 2 * P * (pair + 1))
+            def quantise_hid(pair):
+                x_codes[pair] = work.tile([P, 2 * P], U32, name="x_codes", align_bytes=64)
+                x_plane[pair] = work.tile([P, 2 * P], U8, name="x_plane", align_bytes=64)
                 nc.vector.quantize_mx(
-                    out=codes[:, cols].bitcast(FP8X4),
-                    scales=plane[:, cols],
-                    in_=grouped[pair][:].rearrange("p a r t -> p (a r t)"),
+                    out=x_codes[pair][:].bitcast(FP8X4),
+                    scales=x_plane[pair][:],
+                    in_=x_grouped[pair][:].rearrange("p a r t -> p (a r t)"),
                 )
 
             def hidden_matmul(i):
-                rows = slice(P * i, P * (i + 1))
+                rows = slice(P * (i % 2), P * (i % 2 + 1))
                 u_psum[i] = psum.tile([P, WIDTH], F32, name="u_psum", bufs=3)
                 nc.tensor.matmul_mx(
                     out=u_psum[i][:],
-                    lhsT=x_codes[:, rows].bitcast(FP8X4),
-                    lhsT_scale=x_plane[:, rows],
+                    lhsT=x_codes[i // 2][:, rows].bitcast(FP8X4),
+                    lhsT_scale=x_plane[i // 2][:, rows],
                     rhs=hw_codes[:].bitcast(FP8X4),
                     rhs_scale=hw_plane[:],
                     start=True,
@@ -153,7 +154,7 @@ def tile_deter_pb_t_e_kernel(
                 )
 
             def add_bias(i):
-                u_sb[i] = work.tile([P, PACK, P], F32, name="u_sb", bufs=5)
+                u_sb[i] = work.tile([P, PACK, P], F32, name="u_sb", bufs=6)
                 nc.vector.tensor_tensor(
                     out=u_sb[i][:],
                     in0=u_psum[i][:].rearrange("r (q t) -> r t q", t=PACK),
@@ -197,15 +198,13 @@ def tile_deter_pb_t_e_kernel(
                     nc.tensor.transpose(w_t[i][:, t, :], w_sb[i][:, t, :], ident_f[:])
 
             def silu_and_group(i):
-                if i % 2 == 0:
-                    h_grouped[i // 2] = work.tile([P, 2, P, PACK], BF16, name="h_grouped", align_bytes=64)
                 nc.scalar.activation(
-                    out=h_grouped[i // 2][:, i % 2, :, :],
+                    out=h_grouped[:, i, :, :],
                     in_=w_t[i][:].rearrange("q t r -> q r t"),
                     func=ACT.Silu,
                 )
 
-            for step in range(-4, TILES + 4):
+            for step in range(-4, TILES + 5):
                 if step % 2 == 1 and 0 <= step + 1 < TILES:
                     hidden_matmul(step + 1)
                     hidden_matmul(step + 2)
@@ -216,17 +215,25 @@ def tile_deter_pb_t_e_kernel(
                 if 0 <= step - 1 < TILES:
                     sum_squares(step - 1)
                     inverse_rms(step - 1)
-                if 0 <= step - 2 < TILES:
-                    normalise(step - 2)
-                    transpose_normalised(step - 2)
                 if 0 <= step - 3 < TILES:
-                    silu_and_group(step - 3)
+                    normalise(step - 3)
+                    transpose_normalised(step - 3)
+                if 0 <= step - 5 < TILES:
+                    silu_and_group(step - 5)
                 if step % 2 == 1 and 0 <= (step + 3) // 2 < PAIRS:
                     group_hid((step + 3) // 2)
                 if step % 2 == 0 and 0 <= (step + 2) // 2 < PAIRS:
-                    quantise_pair(x_grouped, x_codes, x_plane, (step + 2) // 2)
-                if step % 2 == 1 and 0 <= (step - 5) // 2 < PAIRS:
-                    quantise_pair(h_grouped, h_codes, h_plane, (step - 5) // 2)
+                    quantise_hid((step + 2) // 2)
+
+            for chunk in range(TILES // CHUNK):
+                rows = slice(CHUNK * P * chunk, CHUNK * P * (chunk + 1))
+                nc.vector.quantize_mx(
+                    out=h_codes[:, rows].bitcast(FP8X4),
+                    scales=h_plane[:, rows],
+                    in_=h_grouped[:, CHUNK * chunk : CHUNK * (chunk + 1), :, :].rearrange(
+                        "p a r t -> p (a r t)"
+                    ),
+                )
 
         with tc.psum_pool(name="psum_gru", bufs=1, reuse_waits="tile") as psum:
             gate_psum, det_t, reset, product, update, cand, mixed, back = {}, {}, {}, {}, {}, {}, {}, {}
@@ -329,13 +336,13 @@ def tile_deter_pb_t_e_kernel(
                     reset_gate(step)
                 if 0 <= step + 1 < UNITS:
                     gate_matmul(step + 1, 0)
-                    gate_matmul(step + 1, 1)
-                if 0 <= step < UNITS:
-                    reset_times_c(step)
-                if 0 <= step + 1 < UNITS:
                     gate_matmul(step + 1, 2)
                 if 0 <= step < UNITS:
                     update_gate(step)
+                if 0 <= step + 1 < UNITS:
+                    gate_matmul(step + 1, 1)
+                if 0 <= step < UNITS:
+                    reset_times_c(step)
                 if 0 <= step - 1 < UNITS:
                     candidate(step - 1)
                 if 0 <= step - OUT_LAG < UNITS:

@@ -23,6 +23,7 @@ CHUNK = 4
 SLICES = WIDTH // P
 UNITS = (TILES // CHUNK) * SLICES
 OUT_LAG = 4
+HIDDEN_ISSUES = 2
 
 FLOPS = 2 * ROWS * WIDTH * (WIDTH + GATES * WIDTH)
 
@@ -143,15 +144,16 @@ def tile_deter_pb_t_e_kernel(
             def hidden_matmul(i):
                 rows = slice(P * (i % 2), P * (i % 2 + 1))
                 u_psum[i] = psum.tile([P, WIDTH], F32, name="u_psum", bufs=3)
-                nc.tensor.matmul_mx(
-                    out=u_psum[i][:],
-                    lhsT=x_codes[i // 2][:, rows].bitcast(FP8X4),
-                    lhsT_scale=x_plane[i // 2][:, rows],
-                    rhs=hw_codes[:].bitcast(FP8X4),
-                    rhs_scale=hw_plane[:],
-                    start=True,
-                    stop=True,
-                )
+                for issue in range(HIDDEN_ISSUES):
+                    nc.tensor.matmul_mx(
+                        out=u_psum[i][:],
+                        lhsT=x_codes[i // 2][:, rows].bitcast(FP8X4),
+                        lhsT_scale=x_plane[i // 2][:, rows],
+                        rhs=hw_codes[:].bitcast(FP8X4),
+                        rhs_scale=hw_plane[:],
+                        start=True,
+                        stop=True,
+                    )
 
             def add_bias(i):
                 u_sb[i] = work.tile([P, PACK, P], F32, name="u_sb", bufs=6)

@@ -23,6 +23,7 @@ CHUNK = 4
 SLICES = WIDTH // P
 UNITS = (TILES // CHUNK) * SLICES
 OUT_LAG = 4
+RMS_GROUP = 4
 HIDDEN_ISSUES = 2
 
 FLOPS = 2 * ROWS * WIDTH * (WIDTH + GATES * WIDTH)
@@ -156,7 +157,7 @@ def tile_deter_pb_t_e_kernel(
                     )
 
             def add_bias(i):
-                u_sb[i] = work.tile([P, PACK, P], F32, name="u_sb", bufs=6)
+                u_sb[i] = work.tile([P, PACK, P], F32, name="u_sb", bufs=9)
                 nc.vector.tensor_tensor(
                     out=u_sb[i][:],
                     in0=u_psum[i][:].rearrange("r (q t) -> r t q", t=PACK),
@@ -173,14 +174,14 @@ def tile_deter_pb_t_e_kernel(
                     accum_out=sum_sq[:, i : i + 1],
                 )
 
-            def inverse_rms(i):
-                one = slice(i, i + 1)
+            def inverse_rms(group):
+                one = slice(RMS_GROUP * group, RMS_GROUP * (group + 1))
                 nc.gpsimd.tensor_scalar(
                     out=mean_sq[:, one], in0=sum_sq[:, one],
                     scalar1=1.0 / WIDTH, scalar2=EPS, op0=ALU.mult, op1=ALU.add,
                 )
                 nc.gpsimd.tensor_tensor(
-                    out=inv_rms[:, one], in0=mean_sq[:, one], in1=minus_half[:], op=ALU.pow
+                    out=inv_rms[:, one], in0=mean_sq[:, one], in1=minus_half[:].to_broadcast([P, RMS_GROUP]), op=ALU.pow
                 )
 
             def normalise(i):
@@ -206,7 +207,7 @@ def tile_deter_pb_t_e_kernel(
                     func=ACT.Silu,
                 )
 
-            for step in range(-4, TILES + 5):
+            for step in range(-4, TILES + 8):
                 if step % 2 == 1 and 0 <= step + 1 < TILES:
                     hidden_matmul(step + 1)
                     hidden_matmul(step + 2)
@@ -216,12 +217,13 @@ def tile_deter_pb_t_e_kernel(
                     add_bias(step)
                 if 0 <= step - 1 < TILES:
                     sum_squares(step - 1)
-                    inverse_rms(step - 1)
-                if 0 <= step - 3 < TILES:
-                    normalise(step - 3)
-                    transpose_normalised(step - 3)
-                if 0 <= step - 5 < TILES:
-                    silu_and_group(step - 5)
+                    if step % RMS_GROUP == 0:
+                        inverse_rms(step // RMS_GROUP - 1)
+                if 0 <= step - 6 < TILES:
+                    normalise(step - 6)
+                    transpose_normalised(step - 6)
+                if 0 <= step - 8 < TILES:
+                    silu_and_group(step - 8)
                 if step % 2 == 1 and 0 <= (step + 3) // 2 < PAIRS:
                     group_hid((step + 3) // 2)
                 if step % 2 == 0 and 0 <= (step + 2) // 2 < PAIRS:

@@ -22,7 +22,9 @@ PAIRS = TILES // 2
 CHUNK = 4
 SLICES = WIDTH // P
 UNITS = (TILES // CHUNK) * SLICES
-OUT_LAG = 4
+HALVES = SLICES // 2
+BACK_LAG = 6
+PERMUTE_STEPS = (16, 20)
 RMS_GROUP = 4
 HIDDEN_ISSUES = 2
 
@@ -52,14 +54,15 @@ def tile_deter_pb_t_e_kernel(
         det_sb = keep.tile([P, TILES, WIDTH], BF16, name="det_sb")
         hw_codes = keep.tile([P, WIDTH], U32, name="hw_codes", align_bytes=64)
         hw_plane = keep.tile([P, WIDTH], U8, name="hw_plane", align_bytes=64)
+        gw_words_in = keep.tile([P, GATES * WIDTH], U32, name="gw_words_in", align_bytes=64)
+        gw_plane_in = keep.tile([P, GATES * WIDTH], U8, name="gw_plane_in", align_bytes=64)
         gw_codes = keep.tile([P, GATES * WIDTH], U32, name="gw_codes", align_bytes=64)
         gw_plane = keep.tile([P, GATES * WIDTH], U8, name="gw_plane", align_bytes=64)
         h_grouped = keep.tile([P, TILES, P, PACK], BF16, name="h_grouped", align_bytes=64)
         h_codes = keep.tile([P, ROWS], U32, name="h_codes", align_bytes=64)
         h_plane = keep.tile([P, ROWS], U8, name="h_plane", align_bytes=64)
         ident_f = keep.tile([P, P], F32, name="ident_f")
-        ident_b = keep.tile([P, P], BF16, name="ident_b")
-        gb_rows = keep.tile([P, P], BF16, name="gb_rows")
+        gb_rows = keep.tile([P, 2 * P], BF16, name="gb_rows")
         gate_bias = keep.tile([P, GATES * SLICES], F32, name="gate_bias")
         hb_all = keep.tile([P, WIDTH], BF16, name="hb_all")
         hg_all = keep.tile([P, WIDTH], BF16, name="hg_all")
@@ -71,16 +74,15 @@ def tile_deter_pb_t_e_kernel(
         minus_half = keep.tile([P, 1], F32, name="minus_half")
 
         nc.vector.memset(hw_plane[:].bitcast(I32), 0)
-        nc.vector.memset(gw_plane[:].bitcast(I32), 0)
+        nc.vector.memset(gw_plane_in[:].bitcast(I32), 0)
         nc.gpsimd.memset(gb_rows[:], 0.0)
         nc.gpsimd.memset(minus_half[:], -0.5)
-        make_identity(nc, ident_b[:])
         make_identity(nc, ident_f[:])
 
         nc.scalar.dma_start(out=hb_all[:], in_=hb1.partition_broadcast(P))
         nc.scalar.dma_start(out=hg_all[:], in_=hg1.partition_broadcast(P))
         nc.sync.dma_start(
-            out=gb_rows[0 : GATES * SLICES, :], in_=gb.rearrange("(a m) -> a m", m=P)
+            out=gb_rows[0 : GATES * HALVES, :], in_=gb.rearrange("(a m) -> a m", m=2 * P)
         )
         nc.sync.dma_start(out=x_sb[:, 0:2, :], in_=hid_rows[:, 0:2, :])
         nc.sync.dma_start(
@@ -94,10 +96,10 @@ def tile_deter_pb_t_e_kernel(
                 out=x_sb[:, first : first + CHUNK, :], in_=hid_rows[:, first : first + CHUNK, :]
             )
         nc.sync.dma_start(
-            out=gw_codes[:].bitcast(I32),
+            out=gw_words_in[:].bitcast(I32),
             in_=gw_words.rearrange("g p n t -> (g p) (n t)").bitcast(I32),
         )
-        load_scale_rows(nc, gw_plane, gw_scales)
+        load_scale_rows(nc, gw_plane_in, gw_scales)
         for first in range(0, TILES, 2 * CHUNK):
             nc.sync.dma_start(
                 out=det_sb[:, first : first + 2 * CHUNK, :],
@@ -108,12 +110,13 @@ def tile_deter_pb_t_e_kernel(
         nc.vector.tensor_copy(out=gain_tq[:], in_=hg_all[:].rearrange("r (q t) -> r t q", t=PACK))
 
         with tc.psum_pool(name="psum_hidden", bufs=1) as psum:
-            gb_t = psum.tile([P, P], BF16, name="gb_t", tag="x_t", bufs=2)
-            nc.tensor.transpose(gb_t[:], gb_rows[:], ident_b[:])
-            nc.vector.tensor_copy(out=gate_bias[:, 0 : 2 * SLICES], in_=gb_t[:, 0 : 2 * SLICES])
+            gb_t = psum.tile([P, P], F32, name="gb_t", tag="x_t", bufs=2)
+            nc.tensor.transpose(gb_t[:], gb_rows[:].bitcast(F32), ident_f[:])
+            gb_cols = gb_t[:].bitcast(BF16)
+            nc.vector.tensor_copy(out=gate_bias[:, 0 : 2 * SLICES], in_=gb_cols[:, 0 : 2 * SLICES])
             nc.vector.tensor_scalar_add(
                 out=gate_bias[:, 2 * SLICES : 3 * SLICES],
-                in0=gb_t[:, 2 * SLICES : 3 * SLICES],
+                in0=gb_cols[:, 2 * SLICES : 3 * SLICES],
                 scalar1=-1.0,
             )
 
@@ -207,6 +210,16 @@ def tile_deter_pb_t_e_kernel(
                     func=ACT.Silu,
                 )
 
+            def permute_gate_columns(e):
+                nc.vector.tensor_copy(
+                    out=gw_codes[:].bitcast(I32).rearrange("p (b e m) -> p b e m", e=2, m=P)[:, :, e, :],
+                    in_=gw_words_in[:].bitcast(I32).rearrange("p (b m e) -> p b m e", e=2, m=P)[:, :, :, e],
+                )
+                nc.vector.tensor_copy(
+                    out=gw_plane[:].rearrange("p (b e m) -> p b e m", e=2, m=P)[:, :, e, :],
+                    in_=gw_plane_in[:].rearrange("p (b m e) -> p b m e", e=2, m=P)[:, :, :, e],
+                )
+
             for step in range(-4, TILES + 8):
                 if step % 2 == 1 and 0 <= step + 1 < TILES:
                     hidden_matmul(step + 1)
@@ -228,6 +241,8 @@ def tile_deter_pb_t_e_kernel(
                     group_hid((step + 3) // 2)
                 if step % 2 == 0 and 0 <= (step + 2) // 2 < PAIRS:
                     quantise_hid((step + 2) // 2)
+                if step in PERMUTE_STEPS:
+                    permute_gate_columns(PERMUTE_STEPS.index(step))
 
             for chunk in range(TILES // CHUNK):
                 rows = slice(CHUNK * P * chunk, CHUNK * P * (chunk + 1))
@@ -261,14 +276,14 @@ def tile_deter_pb_t_e_kernel(
                 column = SLICES * gate + unit % SLICES
                 return gate_bias[:, column : column + 1]
 
-            def transpose_deter(unit):
-                chunk, j = divmod(unit, SLICES)
-                det_t[unit] = psum.tile([P, CHUNK, P], BF16, name="det_t", bufs=2)
+            def transpose_deter(pair):
+                chunk, u = divmod(pair, HALVES)
+                det_t[pair] = psum.tile([P, CHUNK, P], F32, name="det_t", bufs=2)
                 for a in range(CHUNK):
                     nc.tensor.transpose(
-                        det_t[unit][:, a, :],
-                        det_sb[:, CHUNK * chunk + a, P * j : P * (j + 1)],
-                        ident_b[:],
+                        det_t[pair][:, a, :],
+                        det_sb[:, CHUNK * chunk + a, 2 * P * u : 2 * P * (u + 1)].bitcast(F32),
+                        ident_f[:],
                     )
 
             def reset_gate(unit):
@@ -299,12 +314,12 @@ def tile_deter_pb_t_e_kernel(
                 nc.scalar.activation(out=cand[unit][:], in_=product[unit][:], func=ACT.Tanh)
 
             def mix(unit):
-                mixed[unit] = work.tile([P, CHUNK, P], F32, name="mixed", bufs=4)
+                mixed[unit] = work.tile([P, CHUNK, P], F32, name="mixed", bufs=6)
                 diff = work.tile([P, CHUNK * P], F32, name="diff")
                 nc.vector.tensor_tensor(
                     out=diff[:],
                     in0=cand[unit][:],
-                    in1=det_t[unit][:].rearrange("n a r -> n (a r)"),
+                    in1=det_t[unit // 2][:].rearrange("n a r -> n (a r)").bitcast(BF16)[:, unit % 2 :: 2],
                     op=ALU.subtract,
                 )
                 nc.gpsimd.tensor_tensor(
@@ -314,28 +329,40 @@ def tile_deter_pb_t_e_kernel(
                     op=ALU.mult,
                 )
 
-            def transpose_back(unit):
-                back[unit] = psum.tile([P, CHUNK, P], F32, name="back", bufs=2)
-                for a in range(CHUNK):
-                    nc.tensor.transpose(back[unit][:, a, :], mixed[unit][:, a, :], ident_f[:])
+            def transpose_back(pair):
+                for d in range(2):
+                    back[pair, d] = psum.tile([P, 2, 2, P], F32, name="back", bufs=2)
+                    for a in range(2):
+                        for e in range(2):
+                            nc.tensor.transpose(
+                                back[pair, d][:, a, e, :], mixed[2 * pair + e][:, 2 * d + a, :], ident_f[:]
+                            )
 
-            def add_deter_and_store(unit):
-                chunk, j = divmod(unit, SLICES)
-                tiles = slice(CHUNK * chunk, CHUNK * (chunk + 1))
-                cols = slice(P * j, P * (j + 1))
-                result = work.tile([P, CHUNK, P], F32, name="result", bufs=4)
+            def add_deter_and_store(pair, d):
+                chunk, u = divmod(pair, HALVES)
+                tiles = slice(CHUNK * chunk + 2 * d, CHUNK * chunk + 2 * d + 2)
+                cols = slice(2 * P * u, 2 * P * (u + 1))
+                result = work.tile([P, 2, P, 2], F32, name="result", bufs=4)
                 nc.vector.tensor_tensor(
-                    out=result[:], in0=back[unit][:], in1=det_sb[:, tiles, cols], op=ALU.add
+                    out=result[:],
+                    in0=back[pair, d][:].rearrange("r a e m -> r a m e"),
+                    in1=det_sb[:, tiles, cols].rearrange("r a (m e) -> r a m e", e=2),
+                    op=ALU.add,
                 )
-                nc.sync.dma_start(out=out_rows[:, tiles, cols], in_=result[:])
+                nc.sync.dma_start(
+                    out=out_rows[:, tiles, cols], in_=result[:].rearrange("r a m e -> r a (m e)")
+                )
 
-            for step in range(-1, UNITS + OUT_LAG):
+            for step in range(-1, UNITS + BACK_LAG + 1):
+                done, d = divmod(step - BACK_LAG - 1, 2)
+                if 0 <= done < UNITS // 2:
+                    add_deter_and_store(done, d)
                 if 0 <= step - 2 < UNITS:
                     mix(step - 2)
-                if 0 <= step - OUT_LAG < UNITS:
-                    transpose_back(step - OUT_LAG)
-                if 0 <= step - 1 < UNITS:
-                    transpose_deter(step - 1)
+                if step % 2 == 0 and 0 <= step < UNITS:
+                    transpose_deter(step // 2)
+                if step % 2 == 0 and 0 <= step - BACK_LAG < UNITS:
+                    transpose_back((step - BACK_LAG) // 2)
                 if 0 <= step < UNITS:
                     reset_gate(step)
                 if 0 <= step + 1 < UNITS:
@@ -349,5 +376,3 @@ def tile_deter_pb_t_e_kernel(
                     reset_times_c(step)
                 if 0 <= step - 1 < UNITS:
                     candidate(step - 1)
-                if 0 <= step - OUT_LAG < UNITS:
-                    add_deter_and_store(step - OUT_LAG)

@@ -26,6 +26,7 @@ HALVES = SLICES // 2
 BACK_LAG = 6
 PERMUTE_STEPS = (16, 20)
 RMS_GROUP = 4
+RMS_STARTS = (0, *range(RMS_GROUP - 1, TILES, RMS_GROUP))
 HIDDEN_ISSUES = 2
 
 FLOPS = 2 * ROWS * WIDTH * (WIDTH + GATES * WIDTH)
@@ -64,32 +65,38 @@ def tile_deter_pb_t_e_kernel(
         ident_f = keep.tile([P, P], F32, name="ident_f")
         gb_rows = keep.tile([P, 2 * P], BF16, name="gb_rows")
         gate_bias = keep.tile([P, GATES * SLICES], F32, name="gate_bias")
-        hb_all = keep.tile([P, WIDTH], BF16, name="hb_all")
-        hg_all = keep.tile([P, WIDTH], BF16, name="hg_all")
+        hb_row = keep.tile([P, WIDTH], BF16, name="hb_row")
+        hg_row = keep.tile([P, WIDTH], BF16, name="hg_row")
+        ones = keep.tile([P, P], BF16, name="ones")
         bias_tq = keep.tile([P, PACK, P], F32, name="bias_tq")
-        gain_tq = keep.tile([P, PACK, P], F32, name="gain_tq")
         sum_sq = keep.tile([P, TILES], F32, name="sum_sq")
         mean_sq = keep.tile([P, TILES], F32, name="mean_sq")
         inv_rms = keep.tile([P, TILES], F32, name="inv_rms")
         minus_half = keep.tile([P, 1], F32, name="minus_half")
+        table_first = keep.tile([P, 1], F32, name="table_first")
 
+        nc.vector.memset(hb_row[:].bitcast(I32), 0)
+        nc.vector.memset(hg_row[:].bitcast(I32), 0)
         nc.vector.memset(hw_plane[:].bitcast(I32), 0)
+        nc.vector.memset(ones[:], 1.0)
         nc.vector.memset(gw_plane_in[:].bitcast(I32), 0)
-        nc.gpsimd.memset(gb_rows[:], 0.0)
         nc.gpsimd.memset(minus_half[:], -0.5)
         make_identity(nc, ident_f[:])
+        nc.gpsimd.memset(gb_rows[:], 0.0)
 
-        nc.scalar.dma_start(out=hb_all[:], in_=hb1.partition_broadcast(P))
-        nc.scalar.dma_start(out=hg_all[:], in_=hg1.partition_broadcast(P))
-        nc.sync.dma_start(
-            out=gb_rows[0 : GATES * HALVES, :], in_=gb.rearrange("(a m) -> a m", m=2 * P)
-        )
+        nc.scalar.activation(out=table_first[:], in_=minus_half[:], func=ACT.Silu)
+
         nc.sync.dma_start(out=x_sb[:, 0:2, :], in_=hid_rows[:, 0:2, :])
+        nc.sync.dma_start(out=hb_row[0:1, :], in_=hb1.rearrange("(o n) -> o n", o=1))
+        nc.sync.dma_start(out=hg_row[0:1, :], in_=hg1.rearrange("(o n) -> o n", o=1))
         nc.sync.dma_start(
             out=hw_codes[:].bitcast(I32),
             in_=hw1_words.rearrange("g p n t -> (g p) (n t)").bitcast(I32),
         )
         load_scale_rows(nc, hw_plane, hw1_scales)
+        nc.sync.dma_start(
+            out=gb_rows[0 : GATES * HALVES, :], in_=gb.rearrange("(a m) -> a m", m=2 * P)
+        )
         nc.sync.dma_start(out=x_sb[:, 2:CHUNK, :], in_=hid_rows[:, 2:CHUNK, :])
         for first in range(CHUNK, TILES, CHUNK):
             nc.sync.dma_start(
@@ -106,24 +113,36 @@ def tile_deter_pb_t_e_kernel(
                 in_=det_rows[:, first : first + 2 * CHUNK, :],
             )
 
-        nc.vector.tensor_copy(out=bias_tq[:], in_=hb_all[:].rearrange("r (q t) -> r t q", t=PACK))
-        nc.vector.tensor_copy(out=gain_tq[:], in_=hg_all[:].rearrange("r (q t) -> r t q", t=PACK))
-
         with tc.psum_pool(name="psum_hidden", bufs=1) as psum:
-            gb_t = psum.tile([P, P], F32, name="gb_t", tag="x_t", bufs=2)
-            nc.tensor.transpose(gb_t[:], gb_rows[:].bitcast(F32), ident_f[:])
-            gb_cols = gb_t[:].bitcast(BF16)
-            nc.vector.tensor_copy(out=gate_bias[:, 0 : 2 * SLICES], in_=gb_cols[:, 0 : 2 * SLICES])
-            nc.vector.tensor_scalar_add(
-                out=gate_bias[:, 2 * SLICES : 3 * SLICES],
-                in0=gb_cols[:, 2 * SLICES : 3 * SLICES],
-                scalar1=-1.0,
-            )
+            gain_psum = psum.tile([P, PACK, P], F32, name="gain_psum")
+            bias_psum = psum.tile([P, PACK, P], F32, name="bias_psum", tag="w_t", bufs=3)
+            gb_t = psum.tile([P, P], F32, name="gb_t", tag="w_t", bufs=3)
+
+            def spread_constants():
+                for spread, row in ((bias_psum, hb_row), (gain_psum, hg_row)):
+                    nc.tensor.matmul(
+                        out=spread[:],
+                        lhsT=ones[:],
+                        rhs=row[:].rearrange("o (q t) -> o t q", t=PACK),
+                        start=True,
+                        stop=True,
+                    )
+                nc.tensor.transpose(gb_t[:], gb_rows[:].bitcast(F32), ident_f[:])
+
+            def keep_constants():
+                nc.vector.tensor_copy(out=bias_tq[:], in_=bias_psum[:])
+                gb_cols = gb_t[:].bitcast(BF16)
+                nc.vector.tensor_copy(out=gate_bias[:, 0 : 2 * SLICES], in_=gb_cols[:, 0 : 2 * SLICES])
+                nc.vector.tensor_scalar_add(
+                    out=gate_bias[:, 2 * SLICES : 3 * SLICES],
+                    in0=gb_cols[:, 2 * SLICES : 3 * SLICES],
+                    scalar1=-1.0,
+                )
 
             x_t, x_grouped, x_codes, x_plane, u_psum, u_sb, w_sb, w_t = {}, {}, {}, {}, {}, {}, {}, {}
 
             def transpose_hid(pair):
-                x_t[pair] = psum.tile([P, 2, 2, P], F32, name="x_t", bufs=2)
+                x_t[pair] = psum.tile([P, 2, 2, P], F32, name="x_t", bufs=1)
                 for a in range(2):
                     words = x_sb[:, 2 * pair + a, :].bitcast(F32)
                     for v in range(2):
@@ -160,7 +179,7 @@ def tile_deter_pb_t_e_kernel(
                     )
 
             def add_bias(i):
-                u_sb[i] = work.tile([P, PACK, P], F32, name="u_sb", bufs=9)
+                u_sb[i] = work.tile([P, PACK, P], F32, name="u_sb", bufs=11)
                 nc.vector.tensor_tensor(
                     out=u_sb[i][:],
                     in0=u_psum[i][:].rearrange("r (q t) -> r t q", t=PACK),
@@ -177,14 +196,14 @@ def tile_deter_pb_t_e_kernel(
                     accum_out=sum_sq[:, i : i + 1],
                 )
 
-            def inverse_rms(group):
-                one = slice(RMS_GROUP * group, RMS_GROUP * (group + 1))
+            def inverse_rms(first, last):
+                one = slice(first, last + 1)
                 nc.gpsimd.tensor_scalar(
                     out=mean_sq[:, one], in0=sum_sq[:, one],
                     scalar1=1.0 / WIDTH, scalar2=EPS, op0=ALU.mult, op1=ALU.add,
                 )
                 nc.gpsimd.tensor_tensor(
-                    out=inv_rms[:, one], in0=mean_sq[:, one], in1=minus_half[:].to_broadcast([P, RMS_GROUP]), op=ALU.pow
+                    out=inv_rms[:, one], in0=mean_sq[:, one], in1=minus_half[:].to_broadcast([P, last + 1 - first]), op=ALU.pow
                 )
 
             def normalise(i):
@@ -193,7 +212,7 @@ def tile_deter_pb_t_e_kernel(
                     out=w_sb[i][:].rearrange("r t q -> r (t q)"),
                     in0=u_sb[i][:].rearrange("r t q -> r (t q)"),
                     scalar=inv_rms[:, i : i + 1],
-                    in1=gain_tq[:].rearrange("r t q -> r (t q)"),
+                    in1=gain_psum[:].rearrange("r t q -> r (t q)"),
                     op0=ALU.mult,
                     op1=ALU.mult,
                 )
@@ -220,23 +239,27 @@ def tile_deter_pb_t_e_kernel(
                     in_=gw_plane_in[:].rearrange("p (b m e) -> p b m e", e=2, m=P)[:, :, :, e],
                 )
 
-            for step in range(-4, TILES + 8):
+            for step in range(-4, TILES + 9):
                 if step % 2 == 1 and 0 <= step + 1 < TILES:
                     hidden_matmul(step + 1)
                     hidden_matmul(step + 2)
                 if step % 2 == 0 and 0 <= (step + 4) // 2 < PAIRS:
                     transpose_hid((step + 4) // 2)
+                if step == -3:
+                    spread_constants()
+                if step == -1:
+                    keep_constants()
                 if 0 <= step < TILES:
                     add_bias(step)
                 if 0 <= step - 1 < TILES:
                     sum_squares(step - 1)
-                    if step % RMS_GROUP == 0:
-                        inverse_rms(step // RMS_GROUP - 1)
-                if 0 <= step - 6 < TILES:
-                    normalise(step - 6)
-                    transpose_normalised(step - 6)
-                if 0 <= step - 8 < TILES:
-                    silu_and_group(step - 8)
+                    if step in RMS_STARTS or step == TILES:
+                        inverse_rms(max(first for first in RMS_STARTS if first < step), step - 1)
+                if 0 <= step - 7 < TILES:
+                    normalise(step - 7)
+                    transpose_normalised(step - 7)
+                if 0 <= step - 9 < TILES:
+                    silu_and_group(step - 9)
                 if step % 2 == 1 and 0 <= (step + 3) // 2 < PAIRS:
                     group_hid((step + 3) // 2)
                 if step % 2 == 0 and 0 <= (step + 2) // 2 < PAIRS:

@@ -15,11 +15,14 @@ PACK = 4
 ROWS = 4096
 WIDTH = 512
 GATES = 3
+PLANE_STEP = 4
 EPS = 1e-4
 
 TILES = ROWS // P
 PAIRS = TILES // 2
 CHUNK = 4
+CHUNKS = TILES // CHUNK
+EARLY_CHUNKS = 6
 SLICES = WIDTH // P
 UNITS = (TILES // CHUNK) * SLICES
 HALVES = SLICES // 2
@@ -27,7 +30,6 @@ BACK_LAG = 6
 PERMUTE_STEPS = (16, 20)
 RMS_GROUP = 4
 RMS_STARTS = (0, *range(RMS_GROUP - 1, TILES, RMS_GROUP))
-HIDDEN_ISSUES = 2
 
 FLOPS = 2 * ROWS * WIDTH * (WIDTH + GATES * WIDTH)
 
@@ -56,9 +58,9 @@ def tile_deter_pb_t_e_kernel(
         hw_codes = keep.tile([P, WIDTH], U32, name="hw_codes", align_bytes=64)
         hw_plane = keep.tile([P, WIDTH], U8, name="hw_plane", align_bytes=64)
         gw_words_in = keep.tile([P, GATES * WIDTH], U32, name="gw_words_in", align_bytes=64)
-        gw_plane_in = keep.tile([P, GATES * WIDTH], U8, name="gw_plane_in", align_bytes=64)
+        gw_plane_in = keep.tile([P, WIDTH], U8, name="gw_plane_in", align_bytes=64)
         gw_codes = keep.tile([P, GATES * WIDTH], U32, name="gw_codes", align_bytes=64)
-        gw_plane = keep.tile([P, GATES * WIDTH], U8, name="gw_plane", align_bytes=64)
+        gw_plane = keep.tile([P, WIDTH], U8, name="gw_plane", align_bytes=64)
         h_grouped = keep.tile([P, TILES, P, PACK], BF16, name="h_grouped", align_bytes=64)
         h_codes = keep.tile([P, ROWS], U32, name="h_codes", align_bytes=64)
         h_plane = keep.tile([P, ROWS], U8, name="h_plane", align_bytes=64)
@@ -88,16 +90,16 @@ def tile_deter_pb_t_e_kernel(
 
         nc.sync.dma_start(out=x_sb[:, 0:2, :], in_=hid_rows[:, 0:2, :])
         nc.sync.dma_start(out=hb_row[0:1, :], in_=hb1.rearrange("(o n) -> o n", o=1))
-        nc.sync.dma_start(out=hg_row[0:1, :], in_=hg1.rearrange("(o n) -> o n", o=1))
+        nc.sync.dma_start(out=x_sb[:, 2:CHUNK, :], in_=hid_rows[:, 2:CHUNK, :])
         nc.sync.dma_start(
             out=hw_codes[:].bitcast(I32),
             in_=hw1_words.rearrange("g p n t -> (g p) (n t)").bitcast(I32),
         )
         load_scale_rows(nc, hw_plane, hw1_scales)
+        nc.sync.dma_start(out=hg_row[0:1, :], in_=hg1.rearrange("(o n) -> o n", o=1))
         nc.sync.dma_start(
             out=gb_rows[0 : GATES * HALVES, :], in_=gb.rearrange("(a m) -> a m", m=2 * P)
         )
-        nc.sync.dma_start(out=x_sb[:, 2:CHUNK, :], in_=hid_rows[:, 2:CHUNK, :])
         for first in range(CHUNK, TILES, CHUNK):
             nc.sync.dma_start(
                 out=x_sb[:, first : first + CHUNK, :], in_=hid_rows[:, first : first + CHUNK, :]
@@ -106,11 +108,23 @@ def tile_deter_pb_t_e_kernel(
             out=gw_words_in[:].bitcast(I32),
             in_=gw_words.rearrange("g p n t -> (g p) (n t)").bitcast(I32),
         )
-        load_scale_rows(nc, gw_plane_in, gw_scales)
+        for gate in range(GATES):
+            gate_scales = gw_scales[:, :, WIDTH * gate : WIDTH * (gate + 1)]
+            load_scale_rows(nc, gw_plane_in[PLANE_STEP * gate : P, :], gate_scales)
         for first in range(0, TILES, 2 * CHUNK):
             nc.sync.dma_start(
                 out=det_sb[:, first : first + 2 * CHUNK, :],
                 in_=det_rows[:, first : first + 2 * CHUNK, :],
+            )
+
+        def quantise_hidden(chunk):
+            rows = slice(CHUNK * P * chunk, CHUNK * P * (chunk + 1))
+            nc.vector.quantize_mx(
+                out=h_codes[:, rows].bitcast(FP8X4),
+                scales=h_plane[:, rows],
+                in_=h_grouped[:, CHUNK * chunk : CHUNK * (chunk + 1), :, :].rearrange(
+                    "p a r t -> p (a r t)"
+                ),
             )
 
         with tc.psum_pool(name="psum_hidden", bufs=1) as psum:
@@ -118,19 +132,22 @@ def tile_deter_pb_t_e_kernel(
             bias_psum = psum.tile([P, PACK, P], F32, name="bias_psum", tag="w_t", bufs=3)
             gb_t = psum.tile([P, P], F32, name="gb_t", tag="w_t", bufs=3)
 
-            def spread_constants():
-                for spread, row in ((bias_psum, hb_row), (gain_psum, hg_row)):
-                    nc.tensor.matmul(
-                        out=spread[:],
-                        lhsT=ones[:],
-                        rhs=row[:].rearrange("o (q t) -> o t q", t=PACK),
-                        start=True,
-                        stop=True,
-                    )
+            def spread(out, row):
+                nc.tensor.matmul(
+                    out=out[:],
+                    lhsT=ones[:],
+                    rhs=row[:].rearrange("o (q t) -> o t q", t=PACK),
+                    start=True,
+                    stop=True,
+                )
+
+            def keep_hidden_bias():
+                nc.vector.tensor_copy(out=bias_tq[:], in_=bias_psum[:])
+
+            def turn_gate_bias():
                 nc.tensor.transpose(gb_t[:], gb_rows[:].bitcast(F32), ident_f[:])
 
-            def keep_constants():
-                nc.vector.tensor_copy(out=bias_tq[:], in_=bias_psum[:])
+            def keep_gate_bias():
                 gb_cols = gb_t[:].bitcast(BF16)
                 nc.vector.tensor_copy(out=gate_bias[:, 0 : 2 * SLICES], in_=gb_cols[:, 0 : 2 * SLICES])
                 nc.vector.tensor_scalar_add(
@@ -142,7 +159,8 @@ def tile_deter_pb_t_e_kernel(
             x_t, x_grouped, x_codes, x_plane, u_psum, u_sb, w_sb, w_t = {}, {}, {}, {}, {}, {}, {}, {}
 
             def transpose_hid(pair):
-                x_t[pair] = psum.tile([P, 2, 2, P], F32, name="x_t", bufs=1)
+                tag, bufs = ("w_t", 3) if pair == 0 else ("x_t", 1)
+                x_t[pair] = psum.tile([P, 2, 2, P], F32, name="x_t", tag=tag, bufs=bufs)
                 for a in range(2):
                     words = x_sb[:, 2 * pair + a, :].bitcast(F32)
                     for v in range(2):
@@ -167,16 +185,15 @@ def tile_deter_pb_t_e_kernel(
             def hidden_matmul(i):
                 rows = slice(P * (i % 2), P * (i % 2 + 1))
                 u_psum[i] = psum.tile([P, WIDTH], F32, name="u_psum", bufs=3)
-                for issue in range(HIDDEN_ISSUES):
-                    nc.tensor.matmul_mx(
-                        out=u_psum[i][:],
-                        lhsT=x_codes[i // 2][:, rows].bitcast(FP8X4),
-                        lhsT_scale=x_plane[i // 2][:, rows],
-                        rhs=hw_codes[:].bitcast(FP8X4),
-                        rhs_scale=hw_plane[:],
-                        start=True,
-                        stop=True,
-                    )
+                nc.tensor.matmul_mx(
+                    out=u_psum[i][:],
+                    lhsT=x_codes[i // 2][:, rows].bitcast(FP8X4),
+                    lhsT_scale=x_plane[i // 2][:, rows],
+                    rhs=hw_codes[:].bitcast(FP8X4),
+                    rhs_scale=hw_plane[:],
+                    start=True,
+                    stop=True,
+                )
 
             def add_bias(i):
                 u_sb[i] = work.tile([P, PACK, P], F32, name="u_sb", bufs=11)
@@ -245,10 +262,14 @@ def tile_deter_pb_t_e_kernel(
                     hidden_matmul(step + 2)
                 if step % 2 == 0 and 0 <= (step + 4) // 2 < PAIRS:
                     transpose_hid((step + 4) // 2)
-                if step == -3:
-                    spread_constants()
+                if step == -2:
+                    spread(bias_psum, hb_row)
+                if step == 2:
+                    spread(gain_psum, hg_row)
                 if step == -1:
-                    keep_constants()
+                    keep_hidden_bias()
+                if step == 2:
+                    turn_gate_bias()
                 if 0 <= step < TILES:
                     add_bias(step)
                 if 0 <= step - 1 < TILES:
@@ -264,18 +285,13 @@ def tile_deter_pb_t_e_kernel(
                     group_hid((step + 3) // 2)
                 if step % 2 == 0 and 0 <= (step + 2) // 2 < PAIRS:
                     quantise_hid((step + 2) // 2)
+                if step == 4:
+                    keep_gate_bias()
                 if step in PERMUTE_STEPS:
                     permute_gate_columns(PERMUTE_STEPS.index(step))
 
-            for chunk in range(TILES // CHUNK):
-                rows = slice(CHUNK * P * chunk, CHUNK * P * (chunk + 1))
-                nc.vector.quantize_mx(
-                    out=h_codes[:, rows].bitcast(FP8X4),
-                    scales=h_plane[:, rows],
-                    in_=h_grouped[:, CHUNK * chunk : CHUNK * (chunk + 1), :, :].rearrange(
-                        "p a r t -> p (a r t)"
-                    ),
-                )
+            for chunk in range(EARLY_CHUNKS):
+                quantise_hidden(chunk)
 
         with tc.psum_pool(name="psum_gru", bufs=1, reuse_waits="tile") as psum:
             gate_psum, det_t, reset, product, update, cand, mixed, back = {}, {}, {}, {}, {}, {}, {}, {}
@@ -283,12 +299,13 @@ def tile_deter_pb_t_e_kernel(
             def gate_matmul(unit, gate):
                 chunk, j = divmod(unit, SLICES)
                 cols = slice(WIDTH * gate + P * j, WIDTH * gate + P * (j + 1))
+                plane_rows, plane_cols = slice(PLANE_STEP * gate, P), slice(P * j, P * (j + 1))
                 rows = slice(CHUNK * P * chunk, CHUNK * P * (chunk + 1))
                 gate_psum[unit, gate] = psum.tile([P, CHUNK * P], F32, name="gate_psum", bufs=4)
                 nc.tensor.matmul_mx(
                     out=gate_psum[unit, gate][:],
                     lhsT=gw_codes[:, cols].bitcast(FP8X4),
-                    lhsT_scale=gw_plane[:, cols],
+                    lhsT_scale=gw_plane[plane_rows, plane_cols],
                     rhs=h_codes[:, rows].bitcast(FP8X4),
                     rhs_scale=h_plane[:, rows],
                     start=True,
@@ -397,5 +414,7 @@ def tile_deter_pb_t_e_kernel(
                     gate_matmul(step + 1, 1)
                 if 0 <= step < UNITS:
                     reset_times_c(step)
+                if 0 <= step < CHUNKS - EARLY_CHUNKS:
+                    quantise_hidden(EARLY_CHUNKS + step)
                 if 0 <= step - 1 < UNITS:
                     candidate(step - 1)

@@ -26,7 +26,7 @@ EARLY_CHUNKS = 6
 SLICES = WIDTH // P
 UNITS = (TILES // CHUNK) * SLICES
 HALVES = SLICES // 2
-BACK_LAG = 6
+BACK_LAG = 5
 PERMUTE_STEPS = (16, 20)
 RMS_GROUP = 4
 RMS_STARTS = (0, *range(RMS_GROUP - 1, TILES, RMS_GROUP))
@@ -65,6 +65,7 @@ def tile_deter_pb_t_e_kernel(
         h_codes = keep.tile([P, ROWS], U32, name="h_codes", align_bytes=64)
         h_plane = keep.tile([P, ROWS], U8, name="h_plane", align_bytes=64)
         ident_f = keep.tile([P, P], F32, name="ident_f")
+        ident_b = keep.tile([P, P], BF16, name="ident_b")
         gb_rows = keep.tile([P, 2 * P], BF16, name="gb_rows")
         gate_bias = keep.tile([P, GATES * SLICES], F32, name="gate_bias")
         hb_row = keep.tile([P, WIDTH], BF16, name="hb_row")
@@ -85,6 +86,7 @@ def tile_deter_pb_t_e_kernel(
         nc.gpsimd.memset(minus_half[:], -0.5)
         make_identity(nc, ident_f[:])
         nc.gpsimd.memset(gb_rows[:], 0.0)
+        make_identity(nc, ident_b[:])
 
         nc.scalar.activation(out=table_first[:], in_=minus_half[:], func=ACT.Silu)
 
@@ -349,65 +351,98 @@ def tile_deter_pb_t_e_kernel(
                     out=update[unit][:], in_=gate_psum[unit, 2][:], func=ACT.Sigmoid, bias=bias_of(unit, 2)
                 )
 
+            def row_parts(unit):
+                parts = 2 if unit == UNITS - 1 else 1
+                return [slice(h * CHUNK * P // parts, (h + 1) * CHUNK * P // parts) for h in range(parts)]
+
             def candidate(unit):
                 cand[unit] = work.tile([P, CHUNK * P], F32, name="cand")
-                nc.scalar.activation(out=cand[unit][:], in_=product[unit][:], func=ACT.Tanh)
+                for rows in row_parts(unit):
+                    nc.scalar.activation(out=cand[unit][:, rows], in_=product[unit][:, rows], func=ACT.Tanh)
 
             def mix(unit):
-                mixed[unit] = work.tile([P, CHUNK, P], F32, name="mixed", bufs=6)
+                mixed[unit] = work.tile([P, CHUNK, P], F32, name="mixed", bufs=5)
                 diff = work.tile([P, CHUNK * P], F32, name="diff")
-                nc.vector.tensor_tensor(
-                    out=diff[:],
-                    in0=cand[unit][:],
-                    in1=det_t[unit // 2][:].rearrange("n a r -> n (a r)").bitcast(BF16)[:, unit % 2 :: 2],
-                    op=ALU.subtract,
-                )
-                nc.gpsimd.tensor_tensor(
-                    out=mixed[unit][:].rearrange("n a r -> n (a r)"),
-                    in0=update[unit][:],
-                    in1=diff[:],
-                    op=ALU.mult,
-                )
+                det_cols = det_t[unit // 2][:].rearrange("n a r -> n (a r)").bitcast(BF16)[:, unit % 2 :: 2]
+                for rows in row_parts(unit):
+                    nc.vector.tensor_tensor(
+                        out=diff[:, rows], in0=cand[unit][:, rows], in1=det_cols[:, rows], op=ALU.subtract
+                    )
+                    nc.gpsimd.tensor_tensor(
+                        out=mixed[unit][:].rearrange("n a r -> n (a r)")[:, rows],
+                        in0=update[unit][:, rows],
+                        in1=diff[:, rows],
+                        op=ALU.mult,
+                    )
+
+            def empties_by_scalar(pair, d):
+                return pair >= UNITS // 2 - 2 and d == 1
 
             def transpose_back(pair):
                 for d in range(2):
-                    back[pair, d] = psum.tile([P, 2, 2, P], F32, name="back", bufs=2)
+                    tag, bufs = ("gate_psum", 4) if pair >= UNITS // 2 - 2 else ("back", 2)
+                    back[pair, d] = psum.tile([P, 2, 2, P], F32, name="back", tag=tag, bufs=bufs)
+                    adds = empties_by_scalar(pair, d)
+                    if adds:
+                        chunk, u = divmod(pair, HALVES)
+                        for a in range(2):
+                            det_rows_of = det_sb[:, CHUNK * chunk + 2 * d + a, 2 * P * u : 2 * P * (u + 1)]
+                            nc.tensor.matmul(
+                                out=back[pair, d][:, a, :, :],
+                                lhsT=ident_b[:],
+                                rhs=det_rows_of.rearrange("r (m e) -> r e m", e=2),
+                                start=a == 0,
+                                stop=False,
+                            )
                     for a in range(2):
                         for e in range(2):
-                            nc.tensor.transpose(
-                                back[pair, d][:, a, e, :], mixed[2 * pair + e][:, 2 * d + a, :], ident_f[:]
+                            nc.tensor.matmul(
+                                out=back[pair, d][:, a, e, :],
+                                lhsT=mixed[2 * pair + e][:, 2 * d + a, :],
+                                rhs=ident_f[:],
+                                is_transpose=True,
+                                start=not adds,
+                                stop=not adds or (a, e) == (1, 1),
                             )
 
             def add_deter_and_store(pair, d):
                 chunk, u = divmod(pair, HALVES)
                 tiles = slice(CHUNK * chunk + 2 * d, CHUNK * chunk + 2 * d + 2)
                 cols = slice(2 * P * u, 2 * P * (u + 1))
-                result = work.tile([P, 2, P, 2], F32, name="result", bufs=4)
-                nc.vector.tensor_tensor(
-                    out=result[:],
-                    in0=back[pair, d][:].rearrange("r a e m -> r a m e"),
-                    in1=det_sb[:, tiles, cols].rearrange("r a (m e) -> r a m e", e=2),
-                    op=ALU.add,
-                )
+                result = work.tile([P, 2, P, 2], F32, name="result", bufs=7)
+                bank = back[pair, d][:].rearrange("r a e m -> r a m e")
+                if empties_by_scalar(pair, d):
+                    nc.scalar.copy(out=result[:], in_=bank)
+                else:
+                    nc.vector.tensor_tensor(
+                        out=result[:],
+                        in0=bank,
+                        in1=det_sb[:, tiles, cols].rearrange("r a (m e) -> r a m e", e=2),
+                        op=ALU.add,
+                    )
                 nc.sync.dma_start(
                     out=out_rows[:, tiles, cols], in_=result[:].rearrange("r a m e -> r a (m e)")
                 )
 
             for step in range(-1, UNITS + BACK_LAG + 1):
                 done, d = divmod(step - BACK_LAG - 1, 2)
+                if UNITS - 2 <= step - 2 < UNITS:
+                    mix(step - 2)
                 if 0 <= done < UNITS // 2:
                     add_deter_and_store(done, d)
-                if 0 <= step - 2 < UNITS:
+                if 0 <= step - 2 < UNITS - 2:
                     mix(step - 2)
-                if step % 2 == 0 and 0 <= step < UNITS:
+                if step % 2 == 1 and 0 <= step < UNITS:
                     transpose_deter(step // 2)
-                if step % 2 == 0 and 0 <= step - BACK_LAG < UNITS:
+                if step % 2 == 1 and 0 <= step - BACK_LAG < UNITS:
                     transpose_back((step - BACK_LAG) // 2)
                 if 0 <= step < UNITS:
                     reset_gate(step)
                 if 0 <= step + 1 < UNITS:
                     gate_matmul(step + 1, 0)
                     gate_matmul(step + 1, 2)
+                if step == UNITS - 1:
+                    candidate(step - 1)
                 if 0 <= step < UNITS:
                     update_gate(step)
                 if 0 <= step + 1 < UNITS:
@@ -416,5 +451,5 @@ def tile_deter_pb_t_e_kernel(
                     reset_times_c(step)
                 if 0 <= step < CHUNKS - EARLY_CHUNKS:
                     quantise_hidden(EARLY_CHUNKS + step)
-                if 0 <= step - 1 < UNITS:
+                if 0 <= step - 1 < UNITS and step != UNITS - 1:
                     candidate(step - 1)

import concourse.mybir as mybir
from concourse.masks import make_identity

F32 = mybir.dt.float32
BF16 = mybir.dt.bfloat16
I32 = mybir.dt.int32
U32 = mybir.dt.uint32
U8 = mybir.dt.uint8
FP8X4 = mybir.dt.float8_e4m3fn_x4
ACT = mybir.ActivationFunctionType
ALU = mybir.AluOpType

P = 128
PACK = 4
ROWS = 4096
WIDTH = 512
GATES = 3
PLANE_STEP = 4
EPS = 1e-4

TILES = ROWS // P
PAIRS = TILES // 2
CHUNK = 4
CHUNKS = TILES // CHUNK
EARLY_CHUNKS = 6
SLICES = WIDTH // P
UNITS = (TILES // CHUNK) * SLICES
HALVES = SLICES // 2
BACK_LAG = 5
PERMUTE_STEPS = (16, 20)
RMS_GROUP = 4
RMS_STARTS = (0, *range(RMS_GROUP - 1, TILES, RMS_GROUP))

FLOPS = 2 * ROWS * WIDTH * (WIDTH + GATES * WIDTH)


def load_scale_rows(nc, plane, scales):
    for quadrant in range(4):
        nc.sync.dma_start(
            out=plane[32 * quadrant : 32 * quadrant + 4, :].bitcast(I32),
            in_=scales[0, 4 * quadrant : 4 * quadrant + 4, :].bitcast(I32),
        )


def tile_deter_pb_t_e_kernel(
    tc, hid0, deter, hw1_words, hw1_scales, hb1, hg1, gw_words, gw_scales, gb, out
):
    nc = tc.nc
    hid_rows = hid0.rearrange("(r i) k -> r i k", i=TILES)
    det_rows = deter.rearrange("(r i) n -> r i n", i=TILES)
    out_rows = out.rearrange("(r i) n -> r i n", i=TILES)

    with tc.tile_pool(name="keep", bufs=1) as keep, tc.tile_pool(
        name="work", bufs=3
    ) as work, tc.manual_schedule():
        x_sb = keep.tile([P, TILES, WIDTH], BF16, name="x_sb")
        det_sb = keep.tile([P, TILES, WIDTH], BF16, name="det_sb")
        hw_codes = keep.tile([P, WIDTH], U32, name="hw_codes", align_bytes=64)
        hw_plane = keep.tile([P, WIDTH], U8, name="hw_plane", align_bytes=64)
        gw_words_in = keep.tile([P, GATES * WIDTH], U32, name="gw_words_in", align_bytes=64)
        gw_plane_in = keep.tile([P, WIDTH], U8, name="gw_plane_in", align_bytes=64)
        gw_codes = keep.tile([P, GATES * WIDTH], U32, name="gw_codes", align_bytes=64)
        gw_plane = keep.tile([P, WIDTH], U8, name="gw_plane", align_bytes=64)
        h_grouped = keep.tile([P, TILES, P, PACK], BF16, name="h_grouped", align_bytes=64)
        h_codes = keep.tile([P, ROWS], U32, name="h_codes", align_bytes=64)
        h_plane = keep.tile([P, ROWS], U8, name="h_plane", align_bytes=64)
        ident_f = keep.tile([P, P], F32, name="ident_f")
        ident_b = keep.tile([P, P], BF16, name="ident_b")
        gb_rows = keep.tile([P, 2 * P], BF16, name="gb_rows")
        gate_bias = keep.tile([P, GATES * SLICES], F32, name="gate_bias")
        hb_row = keep.tile([P, WIDTH], BF16, name="hb_row")
        hg_row = keep.tile([P, WIDTH], BF16, name="hg_row")
        ones = keep.tile([P, P], BF16, name="ones")
        bias_tq = keep.tile([P, PACK, P], F32, name="bias_tq")
        sum_sq = keep.tile([P, TILES], F32, name="sum_sq")
        mean_sq = keep.tile([P, TILES], F32, name="mean_sq")
        inv_rms = keep.tile([P, TILES], F32, name="inv_rms")
        minus_half = keep.tile([P, 1], F32, name="minus_half")
        table_first = keep.tile([P, 1], F32, name="table_first")

        nc.vector.memset(hb_row[:].bitcast(I32), 0)
        nc.vector.memset(hg_row[:].bitcast(I32), 0)
        nc.vector.memset(hw_plane[:].bitcast(I32), 0)
        nc.vector.memset(ones[:], 1.0)
        nc.vector.memset(gw_plane_in[:].bitcast(I32), 0)
        nc.gpsimd.memset(minus_half[:], -0.5)
        make_identity(nc, ident_f[:])
        nc.gpsimd.memset(gb_rows[:], 0.0)
        make_identity(nc, ident_b[:])

        nc.scalar.activation(out=table_first[:], in_=minus_half[:], func=ACT.Silu)

        nc.sync.dma_start(out=x_sb[:, 0:2, :], in_=hid_rows[:, 0:2, :])
        nc.sync.dma_start(out=hb_row[0:1, :], in_=hb1.rearrange("(o n) -> o n", o=1))
        nc.sync.dma_start(out=x_sb[:, 2:CHUNK, :], in_=hid_rows[:, 2:CHUNK, :])
        nc.sync.dma_start(
            out=hw_codes[:].bitcast(I32),
            in_=hw1_words.rearrange("g p n t -> (g p) (n t)").bitcast(I32),
        )
        load_scale_rows(nc, hw_plane, hw1_scales)
        nc.sync.dma_start(out=hg_row[0:1, :], in_=hg1.rearrange("(o n) -> o n", o=1))
        nc.sync.dma_start(
            out=gb_rows[0 : GATES * HALVES, :], in_=gb.rearrange("(a m) -> a m", m=2 * P)
        )
        for first in range(CHUNK, TILES, CHUNK):
            nc.sync.dma_start(
                out=x_sb[:, first : first + CHUNK, :], in_=hid_rows[:, first : first + CHUNK, :]
            )
        nc.sync.dma_start(
            out=gw_words_in[:].bitcast(I32),
            in_=gw_words.rearrange("g p n t -> (g p) (n t)").bitcast(I32),
        )
        for gate in range(GATES):
            gate_scales = gw_scales[:, :, WIDTH * gate : WIDTH * (gate + 1)]
            load_scale_rows(nc, gw_plane_in[PLANE_STEP * gate : P, :], gate_scales)
        for first in range(0, TILES, 2 * CHUNK):
            nc.sync.dma_start(
                out=det_sb[:, first : first + 2 * CHUNK, :],
                in_=det_rows[:, first : first + 2 * CHUNK, :],
            )

        def quantise_hidden(chunk):
            rows = slice(CHUNK * P * chunk, CHUNK * P * (chunk + 1))
            nc.vector.quantize_mx(
                out=h_codes[:, rows].bitcast(FP8X4),
                scales=h_plane[:, rows],
                in_=h_grouped[:, CHUNK * chunk : CHUNK * (chunk + 1), :, :].rearrange(
                    "p a r t -> p (a r t)"
                ),
            )

        with tc.psum_pool(name="psum_hidden", bufs=1) as psum:
            gain_psum = psum.tile([P, PACK, P], F32, name="gain_psum")
            bias_psum = psum.tile([P, PACK, P], F32, name="bias_psum", tag="w_t", bufs=3)
            gb_t = psum.tile([P, P], F32, name="gb_t", tag="w_t", bufs=3)

            def spread(out, row):
                nc.tensor.matmul(
                    out=out[:],
                    lhsT=ones[:],
                    rhs=row[:].rearrange("o (q t) -> o t q", t=PACK),
                    start=True,
                    stop=True,
                )

            def keep_hidden_bias():
                nc.vector.tensor_copy(out=bias_tq[:], in_=bias_psum[:])

            def turn_gate_bias():
                nc.tensor.transpose(gb_t[:], gb_rows[:].bitcast(F32), ident_f[:])

            def keep_gate_bias():
                gb_cols = gb_t[:].bitcast(BF16)
                nc.vector.tensor_copy(out=gate_bias[:, 0 : 2 * SLICES], in_=gb_cols[:, 0 : 2 * SLICES])
                nc.vector.tensor_scalar_add(
                    out=gate_bias[:, 2 * SLICES : 3 * SLICES],
                    in0=gb_cols[:, 2 * SLICES : 3 * SLICES],
                    scalar1=-1.0,
                )

            x_t, x_grouped, x_codes, x_plane, u_psum, u_sb, w_sb, w_t = {}, {}, {}, {}, {}, {}, {}, {}

            def transpose_hid(pair):
                tag, bufs = ("w_t", 3) if pair == 0 else ("x_t", 1)
                x_t[pair] = psum.tile([P, 2, 2, P], F32, name="x_t", tag=tag, bufs=bufs)
                for a in range(2):
                    words = x_sb[:, 2 * pair + a, :].bitcast(F32)
                    for v in range(2):
                        nc.tensor.transpose(x_t[pair][:, a, v, :], words[:, v : WIDTH // 2 : 2], ident_f[:])

            def group_hid(pair):
                x_grouped[pair] = work.tile([P, 2, P, PACK], BF16, name="x_grouped", align_bytes=64)
                nc.scalar.copy(
                    out=x_grouped[pair][:].bitcast(F32),
                    in_=x_t[pair][:].rearrange("p a v r -> p a r v"),
                )

            def quantise_hid(pair):
                x_codes[pair] = work.tile([P, 2 * P], U32, name="x_codes", align_bytes=64)
                x_plane[pair] = work.tile([P, 2 * P], U8, name="x_plane", align_bytes=64)
                nc.vector.quantize_mx(
                    out=x_codes[pair][:].bitcast(FP8X4),
                    scales=x_plane[pair][:],
                    in_=x_grouped[pair][:].rearrange("p a r t -> p (a r t)"),
                )

            def hidden_matmul(i):
                rows = slice(P * (i % 2), P * (i % 2 + 1))
                u_psum[i] = psum.tile([P, WIDTH], F32, name="u_psum", bufs=3)
                nc.tensor.matmul_mx(
                    out=u_psum[i][:],
                    lhsT=x_codes[i // 2][:, rows].bitcast(FP8X4),
                    lhsT_scale=x_plane[i // 2][:, rows],
                    rhs=hw_codes[:].bitcast(FP8X4),
                    rhs_scale=hw_plane[:],
                    start=True,
                    stop=True,
                )

            def add_bias(i):
                u_sb[i] = work.tile([P, PACK, P], F32, name="u_sb", bufs=11)
                nc.vector.tensor_tensor(
                    out=u_sb[i][:],
                    in0=u_psum[i][:].rearrange("r (q t) -> r t q", t=PACK),
                    in1=bias_tq[:],
                    op=ALU.add,
                )

            def sum_squares(i):
                squares = work.tile([P, WIDTH], BF16, name="squares", bufs=4)
                nc.scalar.activation(
                    out=squares[:],
                    in_=u_sb[i][:].rearrange("r t q -> r (t q)"),
                    func=ACT.Square,
                    accum_out=sum_sq[:, i : i + 1],
                )

            def inverse_rms(first, last):
                one = slice(first, last + 1)
                nc.gpsimd.tensor_scalar(
                    out=mean_sq[:, one], in0=sum_sq[:, one],
                    scalar1=1.0 / WIDTH, scalar2=EPS, op0=ALU.mult, op1=ALU.add,
                )
                nc.gpsimd.tensor_tensor(
                    out=inv_rms[:, one], in0=mean_sq[:, one], in1=minus_half[:].to_broadcast([P, last + 1 - first]), op=ALU.pow
                )

            def normalise(i):
                w_sb[i] = work.tile([P, PACK, P], F32, name="w_sb")
                nc.vector.scalar_tensor_tensor(
                    out=w_sb[i][:].rearrange("r t q -> r (t q)"),
                    in0=u_sb[i][:].rearrange("r t q -> r (t q)"),
                    scalar=inv_rms[:, i : i + 1],
                    in1=gain_psum[:].rearrange("r t q -> r (t q)"),
                    op0=ALU.mult,
                    op1=ALU.mult,
                )

            def transpose_normalised(i):
                w_t[i] = psum.tile([P, PACK, P], F32, name="w_t", bufs=3)
                for t in range(PACK):
                    nc.tensor.transpose(w_t[i][:, t, :], w_sb[i][:, t, :], ident_f[:])

            def silu_and_group(i):
                nc.scalar.activation(
                    out=h_grouped[:, i, :, :],
                    in_=w_t[i][:].rearrange("q t r -> q r t"),
                    func=ACT.Silu,
                )

            def permute_gate_columns(e):
                nc.vector.tensor_copy(
                    out=gw_codes[:].bitcast(I32).rearrange("p (b e m) -> p b e m", e=2, m=P)[:, :, e, :],
                    in_=gw_words_in[:].bitcast(I32).rearrange("p (b m e) -> p b m e", e=2, m=P)[:, :, :, e],
                )
                nc.vector.tensor_copy(
                    out=gw_plane[:].rearrange("p (b e m) -> p b e m", e=2, m=P)[:, :, e, :],
                    in_=gw_plane_in[:].rearrange("p (b m e) -> p b m e", e=2, m=P)[:, :, :, e],
                )

            for step in range(-4, TILES + 9):
                if step % 2 == 1 and 0 <= step + 1 < TILES:
                    hidden_matmul(step + 1)
                    hidden_matmul(step + 2)
                if step % 2 == 0 and 0 <= (step + 4) // 2 < PAIRS:
                    transpose_hid((step + 4) // 2)
                if step == -2:
                    spread(bias_psum, hb_row)
                if step == 2:
                    spread(gain_psum, hg_row)
                if step == -1:
                    keep_hidden_bias()
                if step == 2:
                    turn_gate_bias()
                if 0 <= step < TILES:
                    add_bias(step)
                if 0 <= step - 1 < TILES:
                    sum_squares(step - 1)
                    if step in RMS_STARTS or step == TILES:
                        inverse_rms(max(first for first in RMS_STARTS if first < step), step - 1)
                if 0 <= step - 7 < TILES:
                    normalise(step - 7)
                    transpose_normalised(step - 7)
                if 0 <= step - 9 < TILES:
                    silu_and_group(step - 9)
                if step % 2 == 1 and 0 <= (step + 3) // 2 < PAIRS:
                    group_hid((step + 3) // 2)
                if step % 2 == 0 and 0 <= (step + 2) // 2 < PAIRS:
                    quantise_hid((step + 2) // 2)
                if step == 4:
                    keep_gate_bias()
                if step in PERMUTE_STEPS:
                    permute_gate_columns(PERMUTE_STEPS.index(step))

            for chunk in range(EARLY_CHUNKS):
                quantise_hidden(chunk)

        with tc.psum_pool(name="psum_gru", bufs=1, reuse_waits="tile") as psum:
            gate_psum, det_t, reset, product, update, cand, mixed, back = {}, {}, {}, {}, {}, {}, {}, {}

            def gate_matmul(unit, gate):
                chunk, j = divmod(unit, SLICES)
                cols = slice(WIDTH * gate + P * j, WIDTH * gate + P * (j + 1))
                plane_rows, plane_cols = slice(PLANE_STEP * gate, P), slice(P * j, P * (j + 1))
                rows = slice(CHUNK * P * chunk, CHUNK * P * (chunk + 1))
                gate_psum[unit, gate] = psum.tile([P, CHUNK * P], F32, name="gate_psum", bufs=4)
                nc.tensor.matmul_mx(
                    out=gate_psum[unit, gate][:],
                    lhsT=gw_codes[:, cols].bitcast(FP8X4),
                    lhsT_scale=gw_plane[plane_rows, plane_cols],
                    rhs=h_codes[:, rows].bitcast(FP8X4),
                    rhs_scale=h_plane[:, rows],
                    start=True,
                    stop=True,
                )

            def bias_of(unit, gate):
                column = SLICES * gate + unit % SLICES
                return gate_bias[:, column : column + 1]

            def transpose_deter(pair):
                chunk, u = divmod(pair, HALVES)
                det_t[pair] = psum.tile([P, CHUNK, P], F32, name="det_t", bufs=2)
                for a in range(CHUNK):
                    nc.tensor.transpose(
                        det_t[pair][:, a, :],
                        det_sb[:, CHUNK * chunk + a, 2 * P * u : 2 * P * (u + 1)].bitcast(F32),
                        ident_f[:],
                    )

            def reset_gate(unit):
                reset[unit] = work.tile([P, CHUNK * P], F32, name="reset")
                nc.scalar.activation(
                    out=reset[unit][:], in_=gate_psum[unit, 0][:], func=ACT.Sigmoid, bias=bias_of(unit, 0)
                )

            def reset_times_c(unit):
                product[unit] = work.tile([P, CHUNK * P], F32, name="product")
                nc.vector.scalar_tensor_tensor(
                    out=product[unit][:],
                    in0=gate_psum[unit, 1][:],
                    scalar=bias_of(unit, 1),
                    in1=reset[unit][:],
                    op0=ALU.add,
                    op1=ALU.mult,
                )

            def update_gate(unit):
                update[unit] = work.tile([P, CHUNK * P], F32, name="update", bufs=4)
                nc.scalar.activation(
                    out=update[unit][:], in_=gate_psum[unit, 2][:], func=ACT.Sigmoid, bias=bias_of(unit, 2)
                )

            def row_parts(unit):
                parts = 2 if unit == UNITS - 1 else 1
                return [slice(h * CHUNK * P // parts, (h + 1) * CHUNK * P // parts) for h in range(parts)]

            def candidate(unit):
                cand[unit] = work.tile([P, CHUNK * P], F32, name="cand")
                for rows in row_parts(unit):
                    nc.scalar.activation(out=cand[unit][:, rows], in_=product[unit][:, rows], func=ACT.Tanh)

            def mix(unit):
                mixed[unit] = work.tile([P, CHUNK, P], F32, name="mixed", bufs=5)
                diff = work.tile([P, CHUNK * P], F32, name="diff")
                det_cols = det_t[unit // 2][:].rearrange("n a r -> n (a r)").bitcast(BF16)[:, unit % 2 :: 2]
                for rows in row_parts(unit):
                    nc.vector.tensor_tensor(
                        out=diff[:, rows], in0=cand[unit][:, rows], in1=det_cols[:, rows], op=ALU.subtract
                    )
                    nc.gpsimd.tensor_tensor(
                        out=mixed[unit][:].rearrange("n a r -> n (a r)")[:, rows],
                        in0=update[unit][:, rows],
                        in1=diff[:, rows],
                        op=ALU.mult,
                    )

            def empties_by_scalar(pair, d):
                return pair >= UNITS // 2 - 2 and d == 1

            def transpose_back(pair):
                for d in range(2):
                    tag, bufs = ("gate_psum", 4) if pair >= UNITS // 2 - 2 else ("back", 2)
                    back[pair, d] = psum.tile([P, 2, 2, P], F32, name="back", tag=tag, bufs=bufs)
                    adds = empties_by_scalar(pair, d)
                    if adds:
                        chunk, u = divmod(pair, HALVES)
                        for a in range(2):
                            det_rows_of = det_sb[:, CHUNK * chunk + 2 * d + a, 2 * P * u : 2 * P * (u + 1)]
                            nc.tensor.matmul(
                                out=back[pair, d][:, a, :, :],
                                lhsT=ident_b[:],
                                rhs=det_rows_of.rearrange("r (m e) -> r e m", e=2),
                                start=a == 0,
                                stop=False,
                            )
                    for a in range(2):
                        for e in range(2):
                            nc.tensor.matmul(
                                out=back[pair, d][:, a, e, :],
                                lhsT=mixed[2 * pair + e][:, 2 * d + a, :],
                                rhs=ident_f[:],
                                is_transpose=True,
                                start=not adds,
                                stop=not adds or (a, e) == (1, 1),
                            )

            def add_deter_and_store(pair, d):
                chunk, u = divmod(pair, HALVES)
                tiles = slice(CHUNK * chunk + 2 * d, CHUNK * chunk + 2 * d + 2)
                cols = slice(2 * P * u, 2 * P * (u + 1))
                result = work.tile([P, 2, P, 2], F32, name="result", bufs=7)
                bank = back[pair, d][:].rearrange("r a e m -> r a m e")
                if empties_by_scalar(pair, d):
                    nc.scalar.copy(out=result[:], in_=bank)
                else:
                    nc.vector.tensor_tensor(
                        out=result[:],
                        in0=bank,
                        in1=det_sb[:, tiles, cols].rearrange("r a (m e) -> r a m e", e=2),
                        op=ALU.add,
                    )
                nc.sync.dma_start(
                    out=out_rows[:, tiles, cols], in_=result[:].rearrange("r a m e -> r a (m e)")
                )

            for step in range(-1, UNITS + BACK_LAG + 1):
                done, d = divmod(step - BACK_LAG - 1, 2)
                if UNITS - 2 <= step - 2 < UNITS:
                    mix(step - 2)
                if 0 <= done < UNITS // 2:
                    add_deter_and_store(done, d)
                if 0 <= step - 2 < UNITS - 2:
                    mix(step - 2)
                if step % 2 == 1 and 0 <= step < UNITS:
                    transpose_deter(step // 2)
                if step % 2 == 1 and 0 <= step - BACK_LAG < UNITS:
                    transpose_back((step - BACK_LAG) // 2)
                if 0 <= step < UNITS:
                    reset_gate(step)
                if 0 <= step + 1 < UNITS:
                    gate_matmul(step + 1, 0)
                    gate_matmul(step + 1, 2)
                if step == UNITS - 1:
                    candidate(step - 1)
                if 0 <= step < UNITS:
                    update_gate(step)
                if 0 <= step + 1 < UNITS:
                    gate_matmul(step + 1, 1)
                if 0 <= step < UNITS:
                    reset_times_c(step)
                if 0 <= step < CHUNKS - EARLY_CHUNKS:
                    quantise_hidden(EARLY_CHUNKS + step)
                if 0 <= step - 1 < UNITS and step != UNITS - 1:
                    candidate(step - 1)
